import numpy as np
import ml_dtypes


def mxq(x, axis, fmt="e4m3"):
    dtype, down = {"e4m3": (ml_dtypes.float8_e4m3fn, 7), "e5m2": (ml_dtypes.float8_e5m2, 14)}[fmt]
    v = np.moveaxis(np.asarray(x, np.float32).astype(ml_dtypes.bfloat16).astype(np.float64), axis, -1)
    blocks = v.reshape(v.shape[:-1] + (-1, 32))
    amax = np.abs(blocks).max(-1, keepdims=True)
    byte = np.maximum(np.where(amax > 0, np.frexp(amax)[1] - 1 + 127, 0) - down, 1)
    scale = np.exp2(byte - 127.0)
    codes = (blocks / scale).astype(np.float32).astype(dtype).astype(np.float64)
    return np.moveaxis((codes * scale).reshape(v.shape), -1, axis)


WIDE = False


def mx_kscale(k):
    if not WIDE:
        return np.ones(k)
    levels = np.array([10, -10, 5, -5, 0])
    a = np.random.permutation(np.resize(levels, k // 512 * 4)).reshape(k // 512, 4)
    idx = np.arange(k)
    return np.exp2(a[idx // 512, idx % 128 // 32])


BF16 = ml_dtypes.bfloat16


def bf(x):
    return np.asarray(x, np.float32).astype(BF16)


def f64(x):
    return np.asarray(x).astype(np.float64)


B, H, D, E, S = 1, 8, 256, 512, 1024
HD = H * D


def setup_inputs():
    s = mx_kscale(S)
    return {'v': bf(np.random.standard_normal((B, HD, S)) * s),
            'e_s': bf(np.random.standard_normal((H, B, E, S)) / np.sqrt(S) / s),
            'mask': bf(np.random.uniform(size=(B, 1, S))),
            'regular': bf(1.3 + 0.1 * np.random.standard_normal(1)),
            're_w': bf(np.random.standard_normal((D, HD)) / np.sqrt(HD)),
            're_b': bf(0.1 * np.random.standard_normal(D))}


def reference(v, e_s, mask, regular, re_w, re_b):
    v = f64(v)
    vm = np.concatenate([v[:, :D] * f64(mask) * f64(regular), v[:, D:]], axis=1)
    vh = vm.reshape(B, H, D, S)
    etc_v = mxq(vh, 3, 'e4m3') @ mxq(f64(e_s), 3, 'e4m3').transpose(1, 0, 3, 2)
    etc_k = (mxq(f64(re_w), 1, 'e4m3') @ mxq(etc_v.reshape(B, HD, E), 1, 'e4m3')) + f64(re_b)[None, :, None]
    return etc_v, etc_k

@@ -1,0 +1,239 @@
+from contextlib import ExitStack
+
+import concourse.mybir as mybir
+from concourse.masks import make_identity
+
+BF16 = mybir.dt.bfloat16
+F32 = mybir.dt.float32
+U32 = mybir.dt.uint32
+U8 = mybir.dt.uint8
+FP8X4 = mybir.dt.float8_e4m3fn_x4
+
+P = 128
+PACK = 4
+K_PASS = P * PACK
+HALVES = 2
+PAIR = 2
+
+HEADS = 8
+CHANNELS = 256
+SLOTS = 512
+POSITIONS = 1024
+ALL_CHANNELS = HEADS * CHANNELS
+OUT_CHANNELS = 256
+
+POSITION_PASSES = POSITIONS // K_PASS
+CHANNEL_PASSES = ALL_CHANNELS // K_PASS
+HEADS_PER_PASS = K_PASS // CHANNELS
+UNIT_ROWS = 2 * P
+V_TILES = CHANNELS // P
+E_TILES = SLOTS // P
+O_TILES = OUT_CHANNELS // P
+
+FLOPS = 2 * HEADS * CHANNELS * SLOTS * POSITIONS + 2 * OUT_CHANNELS * ALL_CHANNELS * SLOTS
+
+
+def tile_block_pa_kernel(tc, v, e_s, mask, regular, re_w, re_b, out_0, out_1):
+    nc = tc.nc
+    with ExitStack() as ctx:
+        ctx.enter_context(tc.manual_schedule())
+        once = ctx.enter_context(tc.tile_pool(name="once", bufs=1))
+        inputs = ctx.enter_context(tc.tile_pool(name="inputs", bufs=HEADS))
+        grouping = ctx.enter_context(tc.tile_pool(name="grouping", bufs=4))
+        operands = ctx.enter_context(tc.tile_pool(name="operands", bufs=2))
+        results = ctx.enter_context(tc.tile_pool(name="results", bufs=CHANNEL_PASSES))
+        flipped = ctx.enter_context(tc.psum_pool(name="flipped", bufs=4))
+        step2 = ctx.enter_context(tc.psum_pool(name="step2", bufs=2))
+        step3 = ctx.enter_context(tc.psum_pool(name="step3", bufs=1))
+
+        identity = once.tile([P, P], F32)
+        make_identity(nc, identity[:])
+
+        mask_sb = once.tile([P, POSITION_PASSES, HALVES, PAIR], BF16)
+        nc.scalar.dma_start(
+            out=mask_sb[:],
+            in_=mask[0, 0].rearrange(
+                "(g u p e) -> p g u e", g=POSITION_PASSES, u=HALVES, e=PAIR
+            ),
+        )
+        regular_sb = once.tile([P, 1], BF16)
+        nc.scalar.dma_start(out=regular_sb[:], in_=regular.partition_broadcast(P))
+        bias_sb = once.tile([P, O_TILES], BF16)
+        nc.scalar.dma_start(out=bias_sb[:], in_=re_b.rearrange("(p m) -> p m", m=O_TILES))
+
+        head_order = [h + 1 - 2 * (h % HEADS_PER_PASS) for h in range(HEADS)]
+        v_rows = {}
+        e_rows = {}
+        for h in head_order:
+            v_head = inputs.tile([P, V_TILES, POSITIONS], BF16)
+            nc.sync.dma_start(
+                out=v_head[:],
+                in_=v[0, h * CHANNELS : (h + 1) * CHANNELS, :].rearrange(
+                    "(p i) s -> p i s", i=V_TILES
+                ),
+            )
+            v_rows[h] = v_head
+            e_head = inputs.tile([P, E_TILES, POSITIONS], BF16)
+            nc.sync.dma_start(
+                out=e_head[:], in_=e_s[h, 0].rearrange("(p j) s -> p j s", j=E_TILES)
+            )
+            e_rows[h] = e_head
+        w_rows = once.tile([P, O_TILES, ALL_CHANNELS], BF16)
+        nc.sync.dma_start(out=w_rows[:], in_=re_w.rearrange("(p m) c -> p m c", m=O_TILES))
+
+        def prepare(two_row_tiles, g, codes, scales, head0_factor=None):
+            words = two_row_tiles.bitcast(F32)
+            bank = flipped.tile([P, HALVES, UNIT_ROWS], F32)
+            for u in range(HALVES):
+                block = slice((HALVES * g + u) * P, (HALVES * g + u + 1) * P)
+                for i in range(2):
+                    nc.tensor.transpose(
+                        bank[:, u, i * P : (i + 1) * P], words[:, i, block], identity[:]
+                    )
+            grouped = grouping.tile([P, UNIT_ROWS, PACK], BF16, align_bytes=64)
+            if head0_factor is None:
+                nc.scalar.copy(
+                    out=grouped[:].bitcast(F32), in_=bank[:].rearrange("p u c -> p c u")
+                )
+            else:
+                nc.vector.tensor_tensor(
+                    out=grouped[:].rearrange("p c (u e) -> p c u e", e=PAIR),
+                    in0=bank[:].bitcast(BF16).rearrange("p u (c e) -> p c u e", e=PAIR),
+                    in1=head0_factor.unsqueeze(1).to_broadcast([P, UNIT_ROWS, HALVES, PAIR]),
+                    op=mybir.AluOpType.mult,
+                )
+            nc.vector.quantize_mx(
+                out=codes.bitcast(FP8X4),
+                scales=scales,
+                in_=grouped[:].rearrange("p c t -> p (c t)"),
+            )
+
+        head_operands = {}
+
+        def prepare_head(h):
+            v_codes = operands.tile([P, POSITION_PASSES, CHANNELS], U32, align_bytes=64)
+            v_scales = operands.tile([P, POSITION_PASSES, CHANNELS], U8, align_bytes=64)
+            e_codes = operands.tile([P, POSITION_PASSES, SLOTS], U32, align_bytes=64)
+            e_scales = operands.tile([P, POSITION_PASSES, SLOTS], U8, align_bytes=64)
+            for g in range(POSITION_PASSES):
+                prepare(
+                    v_rows[h][:],
+                    g,
+                    v_codes[:, g, :],
+                    v_scales[:, g, :],
+                    head0_factor=factor[:, g, :, :] if h == 0 else None,
+                )
+            for g in range(POSITION_PASSES):
+                for first in range(0, E_TILES, 2):
+                    columns = slice(first * P, (first + 2) * P)
+                    prepare(
+                        e_rows[h][:, first : first + 2, :],
+                        g,
+                        e_codes[:, g, columns],
+                        e_scales[:, g, columns],
+                    )
+            head_operands[h] = (v_codes, v_scales, e_codes, e_scales)
+
+        w_codes = once.tile([P, CHANNEL_PASSES, OUT_CHANNELS], U32, align_bytes=64)
+        w_scales = once.tile([P, CHANNEL_PASSES, OUT_CHANNELS], U8, align_bytes=64)
+
+        def prepare_weights():
+            for g in range(CHANNEL_PASSES):
+                prepare(w_rows[:], g, w_codes[:, g, :], w_scales[:, g, :])
+
+        pass_tiles = {}
+
+        def multiply_head(h):
+            v_codes, v_scales, e_codes, e_scales = head_operands[h]
+            g3, u = divmod(h, HEADS_PER_PASS)
+            if g3 not in pass_tiles:
+                etc_v_sb = results.tile([P, PACK, SLOTS], F32)
+                etc_v_grouped = results.tile([P, SLOTS, PACK], BF16, align_bytes=64)
+                pass_tiles[g3] = (etc_v_sb, etc_v_grouped)
+            etc_v_sb, etc_v_grouped = pass_tiles[g3]
+            mine = slice(V_TILES * u, V_TILES * (u + 1))
+            for i in range(V_TILES):
+                rows = slice(i * P, (i + 1) * P)
+                acc = step2.tile([P, SLOTS], F32)
+                for g in range(POSITION_PASSES):
+                    nc.tensor.matmul_mx(
+                        out=acc[:],
+                        lhsT=v_codes[:, g, rows].bitcast(FP8X4),
+                        lhsT_scale=v_scales[:, g, rows],
+                        rhs=e_codes[:, g, :].bitcast(FP8X4),
+                        rhs_scale=e_scales[:, g, :],
+                        start=(g == 0),
+                        stop=(g == POSITION_PASSES - 1),
+                    )
+                copy_out = nc.scalar.copy if i == 0 else nc.vector.tensor_copy
+                copy_out(
+                    out=etc_v_sb[:, V_TILES * u + i, :].rearrange("p (r j) -> p r j", j=E_TILES),
+                    in_=acc[:].rearrange("p (j r) -> p r j", j=E_TILES),
+                )
+            nc.sync.dma_start(
+                out=out_0[0, h].rearrange("(p i) e -> p i e", i=V_TILES), in_=etc_v_sb[:, mine, :]
+            )
+            nc.vector.tensor_copy(
+                out=etc_v_grouped[:, :, mine], in_=etc_v_sb[:, mine, :].rearrange("p t e -> p e t")
+            )
+
+        etc_v_codes = once.tile([P, CHANNEL_PASSES, SLOTS], U32, align_bytes=64)
+        etc_v_scales = once.tile([P, CHANNEL_PASSES, SLOTS], U8, align_bytes=64)
+
+        def quantise_etc_v(g3):
+            nc.vector.quantize_mx(
+                out=etc_v_codes[:, g3, :].bitcast(FP8X4),
+                scales=etc_v_scales[:, g3, :],
+                in_=pass_tiles[g3][1][:].rearrange("p e t -> p (e t)"),
+            )
+
+        prepare_head(head_order[0])
+
+        regular_f32 = once.tile([P, 1], F32)
+        nc.vector.tensor_copy(out=regular_f32[:], in_=regular_sb[:])
+        factor = once.tile([P, POSITION_PASSES, HALVES, PAIR], F32)
+        nc.scalar.activation(
+            out=factor[:],
+            in_=mask_sb[:],
+            func=mybir.ActivationFunctionType.Copy,
+            scale=regular_f32[:, 0:1],
+        )
+        bias_f32 = once.tile([P, O_TILES], F32)
+        nc.vector.tensor_copy(out=bias_f32[:], in_=bias_sb[:])
+        for step in range(HEADS):
+            if step + 1 < HEADS:
+                prepare_head(head_order[step + 1])
+            else:
+                prepare_weights()
+            multiply_head(head_order[step])
+            if step % HEADS_PER_PASS == HEADS_PER_PASS - 1:
+                quantise_etc_v(step // HEADS_PER_PASS)
+
+        etc_k_acc = [
+            step3.tile([P, SLOTS], F32, name="etc_k_acc%d" % m) for m in range(O_TILES)
+        ]
+        for g3 in range(CHANNEL_PASSES):
+            for m in range(O_TILES):
+                rows = slice(m * P, (m + 1) * P)
+                nc.tensor.matmul_mx(
+                    out=etc_k_acc[m][:],
+                    lhsT=w_codes[:, g3, rows].bitcast(FP8X4),
+                    lhsT_scale=w_scales[:, g3, rows],
+                    rhs=etc_v_codes[:, g3, :].bitcast(FP8X4),
+                    rhs_scale=etc_v_scales[:, g3, :],
+                    start=(g3 == 0),
+                    stop=(g3 == CHANNEL_PASSES - 1),
+                )
+        etc_k_sb = once.tile([P, O_TILES, SLOTS], F32)
+        nc.scalar.activation(
+            out=etc_k_sb[:, 0, :],
+            in_=etc_k_acc[0][:],
+            func=mybir.ActivationFunctionType.Identity,
+            bias=bias_f32[:, 0:1],
+        )
+        nc.vector.tensor_scalar_add(
+            out=etc_k_sb[:, 1, :], in0=etc_k_acc[1][:], scalar1=bias_f32[:, 1:2]
+        )
+        nc.sync.dma_start(
+            out=out_1[0].rearrange("(p m) e -> p m e", m=O_TILES), in_=etc_k_sb[:]
+        )

@@ -110,66 +110,69 @@ def tile_block_pa_kernel(tc, v, e_s, mask, regular, re_w, re_b, out_0, out_1):
 
         head_operands = {}
 
-        def prepare_head(h):
-            v_codes = operands.tile([P, POSITION_PASSES, CHANNELS], U32, align_bytes=64)
-            v_scales = operands.tile([P, POSITION_PASSES, CHANNELS], U8, align_bytes=64)
-            e_codes = operands.tile([P, POSITION_PASSES, SLOTS], U32, align_bytes=64)
-            e_scales = operands.tile([P, POSITION_PASSES, SLOTS], U8, align_bytes=64)
-            for g in range(POSITION_PASSES):
+        def prepare_head_pass(h, g):
+            if g == 0:
+                v_codes = operands.tile([P, POSITION_PASSES, CHANNELS], U32, align_bytes=64)
+                v_scales = operands.tile([P, POSITION_PASSES, CHANNELS], U8, align_bytes=64)
+                e_codes = operands.tile([P, POSITION_PASSES, SLOTS], U32, align_bytes=64)
+                e_scales = operands.tile([P, POSITION_PASSES, SLOTS], U8, align_bytes=64)
+                head_operands[h] = (v_codes, v_scales, e_codes, e_scales)
+            v_codes, v_scales, e_codes, e_scales = head_operands[h]
+            prepare(
+                v_rows[h][:],
+                g,
+                v_codes[:, g, :],
+                v_scales[:, g, :],
+                head0_factor=factor[:, g, :, :] if h == 0 else None,
+            )
+            for first in range(0, E_TILES, 2):
+                columns = slice(first * P, (first + 2) * P)
                 prepare(
-                    v_rows[h][:],
+                    e_rows[h][:, first : first + 2, :],
                     g,
-                    v_codes[:, g, :],
-                    v_scales[:, g, :],
-                    head0_factor=factor[:, g, :, :] if h == 0 else None,
+                    e_codes[:, g, columns],
+                    e_scales[:, g, columns],
                 )
-            for g in range(POSITION_PASSES):
-                for first in range(0, E_TILES, 2):
-                    columns = slice(first * P, (first + 2) * P)
-                    prepare(
-                        e_rows[h][:, first : first + 2, :],
-                        g,
-                        e_codes[:, g, columns],
-                        e_scales[:, g, columns],
-                    )
-            head_operands[h] = (v_codes, v_scales, e_codes, e_scales)
 
         w_codes = once.tile([P, CHANNEL_PASSES, OUT_CHANNELS], U32, align_bytes=64)
         w_scales = once.tile([P, CHANNEL_PASSES, OUT_CHANNELS], U8, align_bytes=64)
 
-        def prepare_weights():
-            for g in range(CHANNEL_PASSES):
+        def prepare_weight_passes(passes):
+            for g in passes:
                 prepare(w_rows[:], g, w_codes[:, g, :], w_scales[:, g, :])
 
         pass_tiles = {}
 
-        def multiply_head(h):
+        def multiply_tile(h, i):
             v_codes, v_scales, e_codes, e_scales = head_operands[h]
             g3, u = divmod(h, HEADS_PER_PASS)
             if g3 not in pass_tiles:
                 etc_v_sb = results.tile([P, PACK, SLOTS], F32)
                 etc_v_grouped = results.tile([P, SLOTS, PACK], BF16, align_bytes=64)
                 pass_tiles[g3] = (etc_v_sb, etc_v_grouped)
+            etc_v_sb = pass_tiles[g3][0]
+            rows = slice(i * P, (i + 1) * P)
+            acc = step2.tile([P, SLOTS], F32)
+            for g in range(POSITION_PASSES):
+                nc.tensor.matmul_mx(
+                    out=acc[:],
+                    lhsT=v_codes[:, g, rows].bitcast(FP8X4),
+                    lhsT_scale=v_scales[:, g, rows],
+                    rhs=e_codes[:, g, :].bitcast(FP8X4),
+                    rhs_scale=e_scales[:, g, :],
+                    start=(g == 0),
+                    stop=(g == POSITION_PASSES - 1),
+                )
+            copy_out = nc.scalar.copy if i == 0 else nc.vector.tensor_copy
+            copy_out(
+                out=etc_v_sb[:, V_TILES * u + i, :].rearrange("p (r j) -> p r j", j=E_TILES),
+                in_=acc[:].rearrange("p (j r) -> p r j", j=E_TILES),
+            )
+
+        def finish_head(h):
+            g3, u = divmod(h, HEADS_PER_PASS)
             etc_v_sb, etc_v_grouped = pass_tiles[g3]
             mine = slice(V_TILES * u, V_TILES * (u + 1))
-            for i in range(V_TILES):
-                rows = slice(i * P, (i + 1) * P)
-                acc = step2.tile([P, SLOTS], F32)
-                for g in range(POSITION_PASSES):
-                    nc.tensor.matmul_mx(
-                        out=acc[:],
-                        lhsT=v_codes[:, g, rows].bitcast(FP8X4),
-                        lhsT_scale=v_scales[:, g, rows],
-                        rhs=e_codes[:, g, :].bitcast(FP8X4),
-                        rhs_scale=e_scales[:, g, :],
-                        start=(g == 0),
-                        stop=(g == POSITION_PASSES - 1),
-                    )
-                copy_out = nc.scalar.copy if i == 0 else nc.vector.tensor_copy
-                copy_out(
-                    out=etc_v_sb[:, V_TILES * u + i, :].rearrange("p (r j) -> p r j", j=E_TILES),
-                    in_=acc[:].rearrange("p (j r) -> p r j", j=E_TILES),
-                )
             nc.sync.dma_start(
                 out=out_0[0, h].rearrange("(p i) e -> p i e", i=V_TILES), in_=etc_v_sb[:, mine, :]
             )
@@ -187,7 +190,8 @@ def tile_block_pa_kernel(tc, v, e_s, mask, regular, re_w, re_b, out_0, out_1):
                 in_=pass_tiles[g3][1][:].rearrange("p e t -> p (e t)"),
             )
 
-        prepare_head(head_order[0])
+        for g in range(POSITION_PASSES):
+            prepare_head_pass(head_order[0], g)
 
         regular_f32 = once.tile([P, 1], F32)
         nc.vector.tensor_copy(out=regular_f32[:], in_=regular_sb[:])
@@ -201,11 +205,13 @@ def tile_block_pa_kernel(tc, v, e_s, mask, regular, re_w, re_b, out_0, out_1):
         bias_f32 = once.tile([P, O_TILES], F32)
         nc.vector.tensor_copy(out=bias_f32[:], in_=bias_sb[:])
         for step in range(HEADS):
-            if step + 1 < HEADS:
-                prepare_head(head_order[step + 1])
-            else:
-                prepare_weights()
-            multiply_head(head_order[step])
+            for half in range(2):
+                if step + 1 < HEADS:
+                    prepare_head_pass(head_order[step + 1], half)
+                else:
+                    prepare_weight_passes(range(2 * half, 2 * half + 2))
+                multiply_tile(head_order[step], half)
+            finish_head(head_order[step])
             if step % HEADS_PER_PASS == HEADS_PER_PASS - 1:
                 quantise_etc_v(step // HEADS_PER_PASS)
 

@@ -27,8 +27,9 @@ CHANNEL_PASSES = ALL_CHANNELS // K_PASS
 HEADS_PER_PASS = K_PASS // CHANNELS
 UNIT_ROWS = 2 * P
 V_TILES = CHANNELS // P
-E_TILES = SLOTS // P
 O_TILES = OUT_CHANNELS // P
+HALF = SLOTS // 2
+STEP3_ORDER = [1, 0, 2, 3]
 
 FLOPS = 2 * HEADS * CHANNELS * SLOTS * POSITIONS + 2 * OUT_CHANNELS * ALL_CHANNELS * SLOTS
 
@@ -39,207 +40,334 @@ def tile_block_pa_kernel(tc, v, e_s, mask, regular, re_w, re_b, out_0, out_1):
         ctx.enter_context(tc.manual_schedule())
         once = ctx.enter_context(tc.tile_pool(name="once", bufs=1))
         inputs = ctx.enter_context(tc.tile_pool(name="inputs", bufs=HEADS))
-        grouping = ctx.enter_context(tc.tile_pool(name="grouping", bufs=4))
-        operands = ctx.enter_context(tc.tile_pool(name="operands", bufs=2))
+        e_inputs = ctx.enter_context(tc.tile_pool(name="e_inputs", bufs=2 * HEADS))
+        grouping = ctx.enter_context(tc.tile_pool(name="grouping", bufs=10))
+        operands = ctx.enter_context(tc.tile_pool(name="operands", bufs=3))
         results = ctx.enter_context(tc.tile_pool(name="results", bufs=CHANNEL_PASSES))
-        flipped = ctx.enter_context(tc.psum_pool(name="flipped", bufs=4))
+        banks = ctx.enter_context(tc.psum_pool(name="banks", bufs=6))
         step2 = ctx.enter_context(tc.psum_pool(name="step2", bufs=2))
-        step3 = ctx.enter_context(tc.psum_pool(name="step3", bufs=1))
 
         identity = once.tile([P, P], F32)
         make_identity(nc, identity[:])
 
-        mask_sb = once.tile([P, POSITION_PASSES, HALVES, PAIR], BF16)
-        nc.scalar.dma_start(
-            out=mask_sb[:],
-            in_=mask[0, 0].rearrange(
-                "(g u p e) -> p g u e", g=POSITION_PASSES, u=HALVES, e=PAIR
-            ),
-        )
-        regular_sb = once.tile([P, 1], BF16)
-        nc.scalar.dma_start(out=regular_sb[:], in_=regular.partition_broadcast(P))
-        bias_sb = once.tile([P, O_TILES], BF16)
-        nc.scalar.dma_start(out=bias_sb[:], in_=re_b.rearrange("(p m) -> p m", m=O_TILES))
-
-        head_order = [h + 1 - 2 * (h % HEADS_PER_PASS) for h in range(HEADS)]
+        head_order = [2, 3, 0, 1, 4, 5, 6, 7]
+        last_head = head_order[-1]
         v_rows = {}
         e_rows = {}
-        for h in head_order:
-            v_head = inputs.tile([P, V_TILES, POSITIONS], BF16)
-            nc.sync.dma_start(
-                out=v_head[:],
-                in_=v[0, h * CHANNELS : (h + 1) * CHANNELS, :].rearrange(
-                    "(p i) s -> p i s", i=V_TILES
-                ),
-            )
-            v_rows[h] = v_head
-            e_head = inputs.tile([P, E_TILES, POSITIONS], BF16)
-            nc.sync.dma_start(
-                out=e_head[:], in_=e_s[h, 0].rearrange("(p j) s -> p j s", j=E_TILES)
-            )
-            e_rows[h] = e_head
         w_rows = once.tile([P, O_TILES, ALL_CHANNELS], BF16)
-        nc.sync.dma_start(out=w_rows[:], in_=re_w.rearrange("(p m) c -> p m c", m=O_TILES))
+        mask_sb = once.tile([P, POSITION_PASSES, HALVES, PAIR], BF16)
+        regular_sb = once.tile([P, 1], BF16)
+        bias_sb = once.tile([P, O_TILES], BF16)
 
-        def prepare(two_row_tiles, g, codes, scales, head0_factor=None):
-            words = two_row_tiles.bitcast(F32)
-            bank = flipped.tile([P, HALVES, UNIT_ROWS], F32)
-            for u in range(HALVES):
-                block = slice((HALVES * g + u) * P, (HALVES * g + u + 1) * P)
-                for i in range(2):
-                    nc.tensor.transpose(
-                        bank[:, u, i * P : (i + 1) * P], words[:, i, block], identity[:]
-                    )
-            grouped = grouping.tile([P, UNIT_ROWS, PACK], BF16, align_bytes=64)
-            if head0_factor is None:
-                nc.scalar.copy(
-                    out=grouped[:].bitcast(F32), in_=bank[:].rearrange("p u c -> p c u")
+        for place in range(HEADS):
+            h = head_order[place]
+            if place == 1:
+                nc.sync.dma_start(
+                    out=mask_sb[:],
+                    in_=mask[0, 0].rearrange(
+                        "(g u p e) -> p g u e", g=POSITION_PASSES, u=HALVES, e=PAIR
+                    ),
                 )
-            else:
-                nc.vector.tensor_tensor(
-                    out=grouped[:].rearrange("p c (u e) -> p c u e", e=PAIR),
-                    in0=bank[:].bitcast(BF16).rearrange("p u (c e) -> p c u e", e=PAIR),
-                    in1=head0_factor.unsqueeze(1).to_broadcast([P, UNIT_ROWS, HALVES, PAIR]),
-                    op=mybir.AluOpType.mult,
+                nc.sync.dma_start(out=regular_sb[:], in_=regular.partition_broadcast(P))
+            if place == HEADS - 1:
+                nc.sync.dma_start(
+                    out=w_rows[:], in_=re_w.rearrange("(p m) c -> p m c", m=O_TILES)
                 )
-            nc.vector.quantize_mx(
-                out=codes.bitcast(FP8X4),
-                scales=scales,
-                in_=grouped[:].rearrange("p c t -> p (c t)"),
+                nc.sync.dma_start(
+                    out=bias_sb[:], in_=re_b.rearrange("(p m) -> p m", m=O_TILES)
+                )
+            v_head = inputs.tile([P, V_TILES, POSITIONS], BF16)
+            v_source = v[0, h * CHANNELS : (h + 1) * CHANNELS, :].rearrange(
+                "(p i) s -> p i s", i=V_TILES
             )
+            if place == 0:
+                for i in range(V_TILES):
+                    nc.sync.dma_start(out=v_head[:, i, :], in_=v_source[:, i, :])
+            else:
+                nc.sync.dma_start(out=v_head[:], in_=v_source)
+            v_rows[h] = v_head
+            for b in range(2):
+                e_half = e_inputs.tile([P, 2, POSITIONS], BF16)
+                nc.sync.dma_start(
+                    out=e_half[:],
+                    in_=e_s[h, 0, b * HALF : (b + 1) * HALF, :].rearrange(
+                        "(p j) s -> p j s", j=2
+                    ),
+                )
+                e_rows[h, b] = e_half
 
+        regular_f32 = once.tile([P, 1], F32)
+        factor = once.tile([P, POSITION_PASSES, HALVES, PAIR], F32)
+        bias_f32 = once.tile([P, O_TILES], F32)
+
+        w_codes = once.tile([P, CHANNEL_PASSES, OUT_CHANNELS], U32, align_bytes=64)
+        w_scales = once.tile([P, CHANNEL_PASSES, OUT_CHANNELS], U8, align_bytes=64)
+        etc_v_codes = once.tile([P, CHANNEL_PASSES, SLOTS], U32, align_bytes=64)
+        etc_v_scales = once.tile([P, CHANNEL_PASSES, SLOTS], U8, align_bytes=64)
         head_operands = {}
+        pass_tiles = {}
 
-        def prepare_head_pass(h, g):
-            if g == 0:
+        units = []
+        for place in range(HEADS):
+            h = head_order[place]
+            if place == HEADS - 1:
+                units.extend([("w", 0, 0, g) for g in range(CHANNEL_PASSES)])
+            units.extend([("v", h, 0, g) for g in range(POSITION_PASSES)])
+            for b in range(2):
+                units.extend([("e", h, b, g) for g in range(POSITION_PASSES)])
+
+        def unit_rows(kind, h, b):
+            if kind == "v":
+                return v_rows[h]
+            if kind == "e":
+                return e_rows[h, b]
+            return w_rows
+
+        def unit_operand(kind, h, b, g):
+            if kind == "w":
+                return w_codes[:, g, :], w_scales[:, g, :]
+            if h not in head_operands:
                 v_codes = operands.tile([P, POSITION_PASSES, CHANNELS], U32, align_bytes=64)
                 v_scales = operands.tile([P, POSITION_PASSES, CHANNELS], U8, align_bytes=64)
                 e_codes = operands.tile([P, POSITION_PASSES, SLOTS], U32, align_bytes=64)
                 e_scales = operands.tile([P, POSITION_PASSES, SLOTS], U8, align_bytes=64)
                 head_operands[h] = (v_codes, v_scales, e_codes, e_scales)
             v_codes, v_scales, e_codes, e_scales = head_operands[h]
-            prepare(
-                v_rows[h][:],
-                g,
-                v_codes[:, g, :],
-                v_scales[:, g, :],
-                head0_factor=factor[:, g, :, :] if h == 0 else None,
-            )
-            for first in range(0, E_TILES, 2):
-                columns = slice(first * P, (first + 2) * P)
-                prepare(
-                    e_rows[h][:, first : first + 2, :],
-                    g,
-                    e_codes[:, g, columns],
-                    e_scales[:, g, columns],
+            if kind == "v":
+                return v_codes[:, g, :], v_scales[:, g, :]
+            columns = slice(b * HALF, (b + 1) * HALF)
+            return e_codes[:, g, columns], e_scales[:, g, columns]
+
+        def transpose_unit(kind, h, b, g):
+            words = unit_rows(kind, h, b)[:].bitcast(F32)
+            bank = banks.tile([P, HALVES, UNIT_ROWS], F32, tag="bank")
+            for i in range(2):
+                for u in range(HALVES):
+                    block = slice((HALVES * g + u) * P, (HALVES * g + u + 1) * P)
+                    nc.tensor.transpose(
+                        bank[:, u, i * P : (i + 1) * P], words[:, i, block], identity[:]
+                    )
+            return bank
+
+        def group_unit(bank, kind, h, g):
+            grouped = grouping.tile([P, UNIT_ROWS, PACK], BF16, align_bytes=64)
+            if kind == "v" and h == 0:
+                nc.vector.tensor_tensor(
+                    out=grouped[:].rearrange("p c (u e) -> p c u e", e=PAIR),
+                    in0=bank[:].bitcast(BF16).rearrange("p u (c e) -> p c u e", e=PAIR),
+                    in1=factor[:, g, :, :]
+                    .unsqueeze(1)
+                    .to_broadcast([P, UNIT_ROWS, HALVES, PAIR]),
+                    op=mybir.AluOpType.mult,
                 )
+            else:
+                nc.scalar.copy(
+                    out=grouped[:].bitcast(F32), in_=bank[:].rearrange("p u c -> p c u")
+                )
+            return grouped
 
-        w_codes = once.tile([P, CHANNEL_PASSES, OUT_CHANNELS], U32, align_bytes=64)
-        w_scales = once.tile([P, CHANNEL_PASSES, OUT_CHANNELS], U8, align_bytes=64)
+        def quantise(grouped, codes, scales):
+            nc.vector.quantize_mx(
+                out=codes.bitcast(FP8X4),
+                scales=scales,
+                in_=grouped.rearrange("p c t -> p (c t)"),
+            )
 
-        def prepare_weight_passes(passes):
-            for g in passes:
-                prepare(w_rows[:], g, w_codes[:, g, :], w_scales[:, g, :])
-
-        pass_tiles = {}
-
-        def multiply_tile(h, i):
+        def multiply(out, h, b, i):
             v_codes, v_scales, e_codes, e_scales = head_operands[h]
-            g3, u = divmod(h, HEADS_PER_PASS)
-            if g3 not in pass_tiles:
-                etc_v_sb = results.tile([P, PACK, SLOTS], F32)
-                etc_v_grouped = results.tile([P, SLOTS, PACK], BF16, align_bytes=64)
-                pass_tiles[g3] = (etc_v_sb, etc_v_grouped)
-            etc_v_sb = pass_tiles[g3][0]
             rows = slice(i * P, (i + 1) * P)
-            acc = step2.tile([P, SLOTS], F32)
+            columns = slice(b * HALF, (b + 1) * HALF)
             for g in range(POSITION_PASSES):
                 nc.tensor.matmul_mx(
-                    out=acc[:],
+                    out=out,
                     lhsT=v_codes[:, g, rows].bitcast(FP8X4),
                     lhsT_scale=v_scales[:, g, rows],
-                    rhs=e_codes[:, g, :].bitcast(FP8X4),
-                    rhs_scale=e_scales[:, g, :],
+                    rhs=e_codes[:, g, columns].bitcast(FP8X4),
+                    rhs_scale=e_scales[:, g, columns],
                     start=(g == 0),
                     stop=(g == POSITION_PASSES - 1),
                 )
-            copy_out = nc.scalar.copy if i == 0 else nc.vector.tensor_copy
-            copy_out(
-                out=etc_v_sb[:, V_TILES * u + i, :].rearrange("p (r j) -> p r j", j=E_TILES),
-                in_=acc[:].rearrange("p (j r) -> p r j", j=E_TILES),
-            )
 
-        def finish_head(h):
-            g3, u = divmod(h, HEADS_PER_PASS)
-            etc_v_sb, etc_v_grouped = pass_tiles[g3]
-            mine = slice(V_TILES * u, V_TILES * (u + 1))
-            nc.sync.dma_start(
-                out=out_0[0, h].rearrange("(p i) e -> p i e", i=V_TILES), in_=etc_v_sb[:, mine, :]
-            )
-            nc.vector.tensor_copy(
-                out=etc_v_grouped[:, :, mine], in_=etc_v_sb[:, mine, :].rearrange("p t e -> p e t")
-            )
-
-        etc_v_codes = once.tile([P, CHANNEL_PASSES, SLOTS], U32, align_bytes=64)
-        etc_v_scales = once.tile([P, CHANNEL_PASSES, SLOTS], U8, align_bytes=64)
-
-        def quantise_etc_v(g3):
-            nc.vector.quantize_mx(
-                out=etc_v_codes[:, g3, :].bitcast(FP8X4),
-                scales=etc_v_scales[:, g3, :],
-                in_=pass_tiles[g3][1][:].rearrange("p e t -> p (e t)"),
-            )
-
-        for g in range(POSITION_PASSES):
-            prepare_head_pass(head_order[0], g)
-
-        regular_f32 = once.tile([P, 1], F32)
-        nc.vector.tensor_copy(out=regular_f32[:], in_=regular_sb[:])
-        factor = once.tile([P, POSITION_PASSES, HALVES, PAIR], F32)
-        nc.scalar.activation(
-            out=factor[:],
-            in_=mask_sb[:],
-            func=mybir.ActivationFunctionType.Copy,
-            scale=regular_f32[:, 0:1],
-        )
-        bias_f32 = once.tile([P, O_TILES], F32)
-        nc.vector.tensor_copy(out=bias_f32[:], in_=bias_sb[:])
-        for step in range(HEADS):
-            for half in range(2):
-                if step + 1 < HEADS:
-                    prepare_head_pass(head_order[step + 1], half)
+        def result_half(h, b):
+            g3 = h // HEADS_PER_PASS
+            if g3 not in pass_tiles:
+                if g3 == STEP3_ORDER[-1]:
+                    low = once.tile([P, PACK, HALF], F32)
+                    high = once.tile([P, PACK, HALF], F32)
+                    pass_tiles[g3] = (low, high)
                 else:
-                    prepare_weight_passes(range(2 * half, 2 * half + 2))
-                multiply_tile(head_order[step], half)
-            finish_head(head_order[step])
-            if step % HEADS_PER_PASS == HEADS_PER_PASS - 1:
-                quantise_etc_v(step // HEADS_PER_PASS)
+                    etc_v_sb = results.tile([P, PACK, SLOTS], F32)
+                    pass_tiles[g3] = (etc_v_sb,)
+            if g3 == STEP3_ORDER[-1]:
+                return pass_tiles[g3][b][:]
+            return pass_tiles[g3][0][:, :, b * HALF : (b + 1) * HALF]
 
-        etc_k_acc = [
-            step3.tile([P, SLOTS], F32, name="etc_k_acc%d" % m) for m in range(O_TILES)
-        ]
-        for g3 in range(CHANNEL_PASSES):
+        def multiply_half(h, b):
+            acc = step2.tile([P, V_TILES, HALF], F32, tag="acc")
+            for i in range(V_TILES):
+                multiply(acc[:, i, :], h, b, i)
+            return acc
+
+        def copy_out(copy, acc, h, b):
+            first = V_TILES * (h % HEADS_PER_PASS)
+            out = result_half(h, b)[:, first : first + V_TILES, :]
+            copy(
+                out=out.rearrange("p i (r j) -> p i r j", j=2),
+                in_=acc[:].rearrange("p i (j r) -> p i r j", j=2),
+            )
+
+        def store_head(h):
+            first = V_TILES * (h % HEADS_PER_PASS)
+            nc.sync.dma_start(
+                out=out_0[0, h].rearrange("(p i) e -> p i e", i=V_TILES),
+                in_=pass_tiles[h // HEADS_PER_PASS][0][:, first : first + V_TILES, :],
+            )
+
+        def store_half(h, b):
+            first = V_TILES * (h % HEADS_PER_PASS)
+            nc.sync.dma_start(
+                out=out_0[0, h].rearrange("(p i) e -> p i e", i=V_TILES)[
+                    :, :, b * HALF : (b + 1) * HALF
+                ],
+                in_=result_half(h, b)[:, first : first + V_TILES, :],
+            )
+
+        etc_v_grouped = {}
+
+        def regroup(g3, b):
+            half_grouped = results.tile([P, HALF, PACK], BF16, align_bytes=64)
+            nc.vector.tensor_copy(
+                out=half_grouped[:],
+                in_=result_half(g3 * HEADS_PER_PASS, b).rearrange("p t e -> p e t"),
+            )
+            etc_v_grouped[g3, b] = half_grouped
+
+        def quantise_etc_v(g3, b):
+            columns = slice(b * HALF, (b + 1) * HALF)
+            quantise(
+                etc_v_grouped[g3, b][:],
+                etc_v_codes[:, g3, columns],
+                etc_v_scales[:, g3, columns],
+            )
+
+        etc_k_acc = {}
+
+        def multiply_step3(g3, b):
+            columns = slice(b * HALF, (b + 1) * HALF)
             for m in range(O_TILES):
+                if (m, b) not in etc_k_acc:
+                    k_bank = banks.tile([P, HALF], F32, tag="bank")
+                    etc_k_acc[m, b] = k_bank
                 rows = slice(m * P, (m + 1) * P)
                 nc.tensor.matmul_mx(
-                    out=etc_k_acc[m][:],
+                    out=etc_k_acc[m, b][:],
                     lhsT=w_codes[:, g3, rows].bitcast(FP8X4),
                     lhsT_scale=w_scales[:, g3, rows],
-                    rhs=etc_v_codes[:, g3, :].bitcast(FP8X4),
-                    rhs_scale=etc_v_scales[:, g3, :],
-                    start=(g3 == 0),
-                    stop=(g3 == CHANNEL_PASSES - 1),
+                    rhs=etc_v_codes[:, g3, columns].bitcast(FP8X4),
+                    rhs_scale=etc_v_scales[:, g3, columns],
+                    start=(g3 == STEP3_ORDER[0]),
+                    stop=(g3 == STEP3_ORDER[-1]),
                 )
+
         etc_k_sb = once.tile([P, O_TILES, SLOTS], F32)
-        nc.scalar.activation(
-            out=etc_k_sb[:, 0, :],
-            in_=etc_k_acc[0][:],
-            func=mybir.ActivationFunctionType.Identity,
-            bias=bias_f32[:, 0:1],
-        )
-        nc.vector.tensor_scalar_add(
-            out=etc_k_sb[:, 1, :], in0=etc_k_acc[1][:], scalar1=bias_f32[:, 1:2]
-        )
-        nc.sync.dma_start(
-            out=out_1[0].rearrange("(p m) e -> p m e", m=O_TILES), in_=etc_k_sb[:]
-        )
+
+        def finish_step3(b):
+            columns = slice(b * HALF, (b + 1) * HALF)
+            nc.scalar.activation(
+                out=etc_k_sb[:, 0, columns],
+                in_=etc_k_acc[0, b][:],
+                func=mybir.ActivationFunctionType.Identity,
+                bias=bias_f32[:, 0:1],
+            )
+            nc.vector.tensor_scalar_add(
+                out=etc_k_sb[:, 1, columns], in0=etc_k_acc[1, b][:], scalar1=bias_f32[:, 1:2]
+            )
+            nc.sync.dma_start(
+                out=out_1[0].rearrange("(p m) e -> p m e", m=O_TILES)[:, :, columns],
+                in_=etc_k_sb[:, :, columns],
+            )
+
+        multiplies = {}
+        scalar_due = {}
+        vector_due = {}
+        for place in range(HEADS - 1):
+            h = head_order[place]
+            for b in range(2):
+                n = units.index(("e", h, b, POSITION_PASSES - 1)) + 5 + b
+                multiplies.setdefault(n, []).append((h, b))
+                if b == 0 or place in (0, 1):
+                    scalar_due.setdefault(n + 1, []).append((h, b))
+                else:
+                    vector_due.setdefault(n + 1, []).append(("copy", h, b))
+                if place % HEADS_PER_PASS == HEADS_PER_PASS - 1:
+                    vector_due.setdefault(n + 2, []).append(("regroup", h, b))
+                    vector_due.setdefault(n + 3, []).append(("quantise", h, b))
+
+        accs = {}
+        head0_first = units.index(("v", 0, 0, 0))
+        for n in range(len(units)):
+            kind, h, b, g = units[n]
+            if n == head0_first - 4:
+                nc.vector.tensor_copy(out=regular_f32[:], in_=regular_sb[:])
+            if n == head0_first - 2:
+                nc.scalar.activation(
+                    out=factor[:],
+                    in_=mask_sb[:],
+                    func=mybir.ActivationFunctionType.Copy,
+                    scale=regular_f32[:, 0:1],
+                )
+            bank = transpose_unit(kind, h, b, g)
+            for job in multiplies.get(n, []):
+                accs[job] = multiply_half(job[0], job[1])
+            grouped = group_unit(bank, kind, h, g)
+            for job in scalar_due.get(n, []):
+                copy_out(nc.scalar.copy, accs[job], job[0], job[1])
+                if job[1] == 1:
+                    store_head(job[0])
+            codes, scales = unit_operand(kind, h, b, g)
+            quantise(grouped[:], codes, scales)
+            for what, job_h, job_b in vector_due.get(n, []):
+                if what == "copy":
+                    copy_out(nc.vector.tensor_copy, accs[job_h, job_b], job_h, job_b)
+                    if job_h // HEADS_PER_PASS == STEP3_ORDER[-1]:
+                        store_half(job_h, 0)
+                        store_half(job_h, 1)
+                    else:
+                        store_head(job_h)
+                elif what == "regroup":
+                    regroup(job_h // HEADS_PER_PASS, job_b)
+                else:
+                    quantise_etc_v(job_h // HEADS_PER_PASS, job_b)
+
+        nc.vector.tensor_copy(out=bias_f32[:], in_=bias_sb[:])
+        last_g3 = STEP3_ORDER[-1]
+        for g3 in STEP3_ORDER[:-1]:
+            multiply_step3(g3, 0)
+
+        def last_half(b):
+            accs_i = []
+            for i in range(V_TILES):
+                acc_i = step2.tile([P, HALF], F32, tag="acc")
+                multiply(acc_i[:], last_head, b, i)
+                accs_i.append(acc_i)
+            for i in range(V_TILES):
+                t = V_TILES * (last_head % HEADS_PER_PASS) + i
+                copy = nc.scalar.copy if i == 0 else nc.vector.tensor_copy
+                copy(
+                    out=result_half(last_head, b)[:, t, :].rearrange("p (r j) -> p r j", j=2),
+                    in_=accs_i[i][:].rearrange("p (j r) -> p r j", j=2),
+                )
+            store_half(last_head, b)
+
+        last_half(0)
+        for g3 in STEP3_ORDER[:-1]:
+            multiply_step3(g3, 1)
+        regroup(last_g3, 0)
+        last_half(1)
+        quantise_etc_v(last_g3, 0)
+        multiply_step3(last_g3, 0)
+        regroup(last_g3, 1)
+        finish_step3(0)
+        quantise_etc_v(last_g3, 1)
+        multiply_step3(last_g3, 1)
+        finish_step3(1)

@@ -29,7 +29,10 @@ UNIT_ROWS = 2 * P
 V_TILES = CHANNELS // P
 O_TILES = OUT_CHANNELS // P
 HALF = SLOTS // 2
+HEAD_ORDER = [2, 3, 0, 1, 4, 5, 6, 7]
 STEP3_ORDER = [1, 0, 2, 3]
+UNITS_PER_HEAD = 6
+AHEAD = 3
 
 FLOPS = 2 * HEADS * CHANNELS * SLOTS * POSITIONS + 2 * OUT_CHANNELS * ALL_CHANNELS * SLOTS
 
@@ -50,17 +53,12 @@ def tile_block_pa_kernel(tc, v, e_s, mask, regular, re_w, re_b, out_0, out_1):
         identity = once.tile([P, P], F32)
         make_identity(nc, identity[:])
 
-        head_order = [2, 3, 0, 1, 4, 5, 6, 7]
-        last_head = head_order[-1]
         v_rows = {}
         e_rows = {}
-        w_rows = once.tile([P, O_TILES, ALL_CHANNELS], BF16)
         mask_sb = once.tile([P, POSITION_PASSES, HALVES, PAIR], BF16)
         regular_sb = once.tile([P, 1], BF16)
-        bias_sb = once.tile([P, O_TILES], BF16)
-
         for place in range(HEADS):
-            h = head_order[place]
+            h = HEAD_ORDER[place]
             if place == 1:
                 nc.sync.dma_start(
                     out=mask_sb[:],
@@ -69,20 +67,14 @@ def tile_block_pa_kernel(tc, v, e_s, mask, regular, re_w, re_b, out_0, out_1):
                     ),
                 )
                 nc.sync.dma_start(out=regular_sb[:], in_=regular.partition_broadcast(P))
-            if place == HEADS - 1:
-                nc.sync.dma_start(
-                    out=w_rows[:], in_=re_w.rearrange("(p m) c -> p m c", m=O_TILES)
-                )
-                nc.sync.dma_start(
-                    out=bias_sb[:], in_=re_b.rearrange("(p m) -> p m", m=O_TILES)
-                )
             v_head = inputs.tile([P, V_TILES, POSITIONS], BF16)
             v_source = v[0, h * CHANNELS : (h + 1) * CHANNELS, :].rearrange(
                 "(p i) s -> p i s", i=V_TILES
             )
             if place == 0:
-                for i in range(V_TILES):
-                    nc.sync.dma_start(out=v_head[:, i, :], in_=v_source[:, i, :])
+                for g in range(POSITION_PASSES):
+                    columns = slice(g * K_PASS, (g + 1) * K_PASS)
+                    nc.sync.dma_start(out=v_head[:, :, columns], in_=v_source[:, :, columns])
             else:
                 nc.sync.dma_start(out=v_head[:], in_=v_source)
             v_rows[h] = v_head
@@ -95,61 +87,51 @@ def tile_block_pa_kernel(tc, v, e_s, mask, regular, re_w, re_b, out_0, out_1):
                     ),
                 )
                 e_rows[h, b] = e_half
+        w_rows = once.tile([P, O_TILES, ALL_CHANNELS], BF16)
+        nc.sync.dma_start(out=w_rows[:], in_=re_w.rearrange("(p m) c -> p m c", m=O_TILES))
+        bias_sb = once.tile([P, O_TILES], BF16)
+        nc.sync.dma_start(out=bias_sb[:], in_=re_b.rearrange("(p m) -> p m", m=O_TILES))
 
         regular_f32 = once.tile([P, 1], F32)
         factor = once.tile([P, POSITION_PASSES, HALVES, PAIR], F32)
         bias_f32 = once.tile([P, O_TILES], F32)
-
         w_codes = once.tile([P, CHANNEL_PASSES, OUT_CHANNELS], U32, align_bytes=64)
         w_scales = once.tile([P, CHANNEL_PASSES, OUT_CHANNELS], U8, align_bytes=64)
         etc_v_codes = once.tile([P, CHANNEL_PASSES, SLOTS], U32, align_bytes=64)
         etc_v_scales = once.tile([P, CHANNEL_PASSES, SLOTS], U8, align_bytes=64)
+        etc_k_sb = once.tile([P, O_TILES, SLOTS], F32)
         head_operands = {}
-        pass_tiles = {}
+        results_of_pass = {}
+        flipped = {}
+        grouped_units = {}
+        accs = {}
+        grouped_etc_v = {}
+        etc_k_acc = {}
 
         units = []
-        for place in range(HEADS):
-            h = head_order[place]
-            if place == HEADS - 1:
-                units.extend([("w", 0, 0, g) for g in range(CHANNEL_PASSES)])
+        for h in HEAD_ORDER:
             units.extend([("v", h, 0, g) for g in range(POSITION_PASSES)])
             for b in range(2):
                 units.extend([("e", h, b, g) for g in range(POSITION_PASSES)])
+        first_w = len(units)
+        units.extend([("w", 0, 0, g) for g in STEP3_ORDER])
 
-        def unit_rows(kind, h, b):
-            if kind == "v":
-                return v_rows[h]
-            if kind == "e":
-                return e_rows[h, b]
-            return w_rows
-
-        def unit_operand(kind, h, b, g):
-            if kind == "w":
-                return w_codes[:, g, :], w_scales[:, g, :]
-            if h not in head_operands:
-                v_codes = operands.tile([P, POSITION_PASSES, CHANNELS], U32, align_bytes=64)
-                v_scales = operands.tile([P, POSITION_PASSES, CHANNELS], U8, align_bytes=64)
-                e_codes = operands.tile([P, POSITION_PASSES, SLOTS], U32, align_bytes=64)
-                e_scales = operands.tile([P, POSITION_PASSES, SLOTS], U8, align_bytes=64)
-                head_operands[h] = (v_codes, v_scales, e_codes, e_scales)
-            v_codes, v_scales, e_codes, e_scales = head_operands[h]
-            if kind == "v":
-                return v_codes[:, g, :], v_scales[:, g, :]
-            columns = slice(b * HALF, (b + 1) * HALF)
-            return e_codes[:, g, columns], e_scales[:, g, columns]
-
-        def transpose_unit(kind, h, b, g):
-            words = unit_rows(kind, h, b)[:].bitcast(F32)
+        def transpose_unit(n):
+            kind, h, b, g = units[n]
+            rows = v_rows[h] if kind == "v" else e_rows[h, b] if kind == "e" else w_rows
+            words = rows[:].bitcast(F32)
             bank = banks.tile([P, HALVES, UNIT_ROWS], F32, tag="bank")
-            for i in range(2):
-                for u in range(HALVES):
-                    block = slice((HALVES * g + u) * P, (HALVES * g + u + 1) * P)
+            for u in range(HALVES):
+                block = slice((HALVES * g + u) * P, (HALVES * g + u + 1) * P)
+                for i in range(2):
                     nc.tensor.transpose(
                         bank[:, u, i * P : (i + 1) * P], words[:, i, block], identity[:]
                     )
-            return bank
+            flipped[n] = bank
 
-        def group_unit(bank, kind, h, g):
+        def group_unit(n):
+            kind, h, b, g = units[n]
+            bank = flipped[n]
             grouped = grouping.tile([P, UNIT_ROWS, PACK], BF16, align_bytes=64)
             if kind == "v" and h == 0:
                 nc.vector.tensor_tensor(
@@ -164,14 +146,32 @@ def tile_block_pa_kernel(tc, v, e_s, mask, regular, re_w, re_b, out_0, out_1):
                 nc.scalar.copy(
                     out=grouped[:].bitcast(F32), in_=bank[:].rearrange("p u c -> p c u")
                 )
-            return grouped
+            grouped_units[n] = grouped
 
         def quantise(grouped, codes, scales):
             nc.vector.quantize_mx(
                 out=codes.bitcast(FP8X4),
                 scales=scales,
-                in_=grouped.rearrange("p c t -> p (c t)"),
+                in_=grouped[:].rearrange("p c t -> p (c t)"),
             )
+
+        def quantise_unit(n):
+            kind, h, b, g = units[n]
+            if kind == "w":
+                quantise(grouped_units[n], w_codes[:, g, :], w_scales[:, g, :])
+                return
+            if h not in head_operands:
+                v_codes = operands.tile([P, POSITION_PASSES, CHANNELS], U32, align_bytes=64)
+                v_scales = operands.tile([P, POSITION_PASSES, CHANNELS], U8, align_bytes=64)
+                e_codes = operands.tile([P, POSITION_PASSES, SLOTS], U32, align_bytes=64)
+                e_scales = operands.tile([P, POSITION_PASSES, SLOTS], U8, align_bytes=64)
+                head_operands[h] = (v_codes, v_scales, e_codes, e_scales)
+            v_codes, v_scales, e_codes, e_scales = head_operands[h]
+            if kind == "v":
+                quantise(grouped_units[n], v_codes[:, g, :], v_scales[:, g, :])
+            else:
+                columns = slice(b * HALF, (b + 1) * HALF)
+                quantise(grouped_units[n], e_codes[:, g, columns], e_scales[:, g, columns])
 
         def multiply(out, h, b, i):
             v_codes, v_scales, e_codes, e_scales = head_operands[h]
@@ -188,39 +188,53 @@ def tile_block_pa_kernel(tc, v, e_s, mask, regular, re_w, re_b, out_0, out_1):
                     stop=(g == POSITION_PASSES - 1),
                 )
 
-        def result_half(h, b):
-            g3 = h // HEADS_PER_PASS
-            if g3 not in pass_tiles:
-                if g3 == STEP3_ORDER[-1]:
-                    low = once.tile([P, PACK, HALF], F32)
-                    high = once.tile([P, PACK, HALF], F32)
-                    pass_tiles[g3] = (low, high)
-                else:
-                    etc_v_sb = results.tile([P, PACK, SLOTS], F32)
-                    pass_tiles[g3] = (etc_v_sb,)
-            if g3 == STEP3_ORDER[-1]:
-                return pass_tiles[g3][b][:]
-            return pass_tiles[g3][0][:, :, b * HALF : (b + 1) * HALF]
-
         def multiply_half(h, b):
             acc = step2.tile([P, V_TILES, HALF], F32, tag="acc")
             for i in range(V_TILES):
                 multiply(acc[:, i, :], h, b, i)
-            return acc
+            accs[h, b] = acc
 
-        def copy_out(copy, acc, h, b):
+        def multiply_half_apart(h, b):
+            for i in range(V_TILES):
+                acc = step2.tile([P, HALF], F32, tag="acc")
+                multiply(acc[:], h, b, i)
+                accs[h, b, i] = acc
+
+        def result_half(h, b):
+            g3 = h // HEADS_PER_PASS
+            if g3 not in results_of_pass:
+                if g3 == STEP3_ORDER[-1]:
+                    low = once.tile([P, PACK, HALF], F32)
+                    high = once.tile([P, PACK, HALF], F32)
+                    results_of_pass[g3] = (low, high)
+                else:
+                    whole = results.tile([P, PACK, SLOTS], F32)
+                    results_of_pass[g3] = (whole,)
+            if g3 == STEP3_ORDER[-1]:
+                return results_of_pass[g3][b][:]
+            return results_of_pass[g3][0][:, :, b * HALF : (b + 1) * HALF]
+
+        def copy_out(copy, h, b):
             first = V_TILES * (h % HEADS_PER_PASS)
-            out = result_half(h, b)[:, first : first + V_TILES, :]
             copy(
-                out=out.rearrange("p i (r j) -> p i r j", j=2),
-                in_=acc[:].rearrange("p i (j r) -> p i r j", j=2),
+                out=result_half(h, b)[:, first : first + V_TILES, :].rearrange(
+                    "p i (r j) -> p i r j", j=2
+                ),
+                in_=accs[h, b][:].rearrange("p i (j r) -> p i r j", j=2),
+            )
+
+        def copy_out_tile(copy, h, b, i):
+            t = V_TILES * (h % HEADS_PER_PASS) + i
+            copy(
+                out=result_half(h, b)[:, t, :].rearrange("p (r j) -> p r j", j=2),
+                in_=accs[h, b, i][:].rearrange("p (j r) -> p r j", j=2),
             )
 
         def store_head(h):
             first = V_TILES * (h % HEADS_PER_PASS)
             nc.sync.dma_start(
                 out=out_0[0, h].rearrange("(p i) e -> p i e", i=V_TILES),
-                in_=pass_tiles[h // HEADS_PER_PASS][0][:, first : first + V_TILES, :],
+                in_=results_of_pass[h // HEADS_PER_PASS][0][:, first : first + V_TILES, :],
             )
 
         def store_half(h, b):
@@ -232,25 +246,19 @@ def tile_block_pa_kernel(tc, v, e_s, mask, regular, re_w, re_b, out_0, out_1):
                 in_=result_half(h, b)[:, first : first + V_TILES, :],
             )
 
-        etc_v_grouped = {}
-
         def regroup(g3, b):
             half_grouped = results.tile([P, HALF, PACK], BF16, align_bytes=64)
             nc.vector.tensor_copy(
                 out=half_grouped[:],
                 in_=result_half(g3 * HEADS_PER_PASS, b).rearrange("p t e -> p e t"),
             )
-            etc_v_grouped[g3, b] = half_grouped
+            grouped_etc_v[g3, b] = half_grouped
 
         def quantise_etc_v(g3, b):
             columns = slice(b * HALF, (b + 1) * HALF)
             quantise(
-                etc_v_grouped[g3, b][:],
-                etc_v_codes[:, g3, columns],
-                etc_v_scales[:, g3, columns],
+                grouped_etc_v[g3, b], etc_v_codes[:, g3, columns], etc_v_scales[:, g3, columns]
             )
-
-        etc_k_acc = {}
 
         def multiply_step3(g3, b):
             columns = slice(b * HALF, (b + 1) * HALF)
@@ -269,8 +277,6 @@ def tile_block_pa_kernel(tc, v, e_s, mask, regular, re_w, re_b, out_0, out_1):
                     stop=(g3 == STEP3_ORDER[-1]),
                 )
 
-        etc_k_sb = once.tile([P, O_TILES, SLOTS], F32)
-
         def finish_step3(b):
             columns = slice(b * HALF, (b + 1) * HALF)
             nc.scalar.activation(
@@ -287,87 +293,72 @@ def tile_block_pa_kernel(tc, v, e_s, mask, regular, re_w, re_b, out_0, out_1):
                 in_=etc_k_sb[:, :, columns],
             )
 
-        multiplies = {}
-        scalar_due = {}
-        vector_due = {}
-        for place in range(HEADS - 1):
-            h = head_order[place]
+        def make_factor():
+            nc.scalar.activation(
+                out=factor[:],
+                in_=mask_sb[:],
+                func=mybir.ActivationFunctionType.Copy,
+                scale=regular_f32[:, 0:1],
+            )
+
+        due = {}
+
+        def later(engine, n, job, *args):
+            due.setdefault((engine, n), []).append((job, args))
+
+        def run_due(engine, n):
+            for job, args in due.get((engine, n), []):
+                job(*args)
+
+        for place in range(HEADS):
+            h = HEAD_ORDER[place]
+            g3 = h // HEADS_PER_PASS
+            end = UNITS_PER_HEAD * (place + 1)
+            if place == HEADS - 1:
+                for b in range(2):
+                    later("tensor", end - 1 + b, multiply_half_apart, h, b)
+                    later("scalar", end + b, copy_out_tile, nc.scalar.copy, h, b, 0)
+                    later("vector", end - 1 + b, copy_out_tile, nc.vector.tensor_copy, h, b, 1)
+                    later("vector", end + b, store_half, h, b)
+                    later("vector", end + b, regroup, g3, b)
+                    later("vector", end + 2 + b, quantise_etc_v, g3, b)
+                continue
             for b in range(2):
-                n = units.index(("e", h, b, POSITION_PASSES - 1)) + 5 + b
-                multiplies.setdefault(n, []).append((h, b))
-                if b == 0 or place in (0, 1):
-                    scalar_due.setdefault(n + 1, []).append((h, b))
-                else:
-                    vector_due.setdefault(n + 1, []).append(("copy", h, b))
-                if place % HEADS_PER_PASS == HEADS_PER_PASS - 1:
-                    vector_due.setdefault(n + 2, []).append(("regroup", h, b))
-                    vector_due.setdefault(n + 3, []).append(("quantise", h, b))
-
-        accs = {}
+                later("tensor", end - 1 + 3 * b, multiply_half, h, b)
+            later("scalar", end + 1, copy_out, nc.scalar.copy, h, 0)
+            if place < 2:
+                later("scalar", end + 4, copy_out, nc.scalar.copy, h, 1)
+            else:
+                later("vector", end + 4, copy_out, nc.vector.tensor_copy, h, 1)
+            if g3 == STEP3_ORDER[-1]:
+                for b in range(2):
+                    later("vector", end + 4, store_half, h, b)
+            else:
+                later("vector", end + 4, store_head, h)
+            if place % HEADS_PER_PASS == HEADS_PER_PASS - 1:
+                for b in range(2):
+                    later("vector", end + 5 + 2 * b, regroup, g3, b)
+                    later("vector", end + 6 + 2 * b, quantise_etc_v, g3, b)
         head0_first = units.index(("v", 0, 0, 0))
+        later("vector", head0_first - 4, nc.vector.tensor_copy, regular_f32[:], regular_sb[:])
+        later("scalar", head0_first - 2, make_factor)
+        later("vector", first_w, nc.vector.tensor_copy, bias_f32[:], bias_sb[:])
+        for b in range(2):
+            later("tensor", first_w + 2, multiply_step3, STEP3_ORDER[0], b)
+            later("tensor", first_w + 3, multiply_step3, STEP3_ORDER[1], b)
+
+        for n in range(AHEAD):
+            transpose_unit(n)
         for n in range(len(units)):
-            kind, h, b, g = units[n]
-            if n == head0_first - 4:
-                nc.vector.tensor_copy(out=regular_f32[:], in_=regular_sb[:])
-            if n == head0_first - 2:
-                nc.scalar.activation(
-                    out=factor[:],
-                    in_=mask_sb[:],
-                    func=mybir.ActivationFunctionType.Copy,
-                    scale=regular_f32[:, 0:1],
-                )
-            bank = transpose_unit(kind, h, b, g)
-            for job in multiplies.get(n, []):
-                accs[job] = multiply_half(job[0], job[1])
-            grouped = group_unit(bank, kind, h, g)
-            for job in scalar_due.get(n, []):
-                copy_out(nc.scalar.copy, accs[job], job[0], job[1])
-                if job[1] == 1:
-                    store_head(job[0])
-            codes, scales = unit_operand(kind, h, b, g)
-            quantise(grouped[:], codes, scales)
-            for what, job_h, job_b in vector_due.get(n, []):
-                if what == "copy":
-                    copy_out(nc.vector.tensor_copy, accs[job_h, job_b], job_h, job_b)
-                    if job_h // HEADS_PER_PASS == STEP3_ORDER[-1]:
-                        store_half(job_h, 0)
-                        store_half(job_h, 1)
-                    else:
-                        store_head(job_h)
-                elif what == "regroup":
-                    regroup(job_h // HEADS_PER_PASS, job_b)
-                else:
-                    quantise_etc_v(job_h // HEADS_PER_PASS, job_b)
-
-        nc.vector.tensor_copy(out=bias_f32[:], in_=bias_sb[:])
-        last_g3 = STEP3_ORDER[-1]
-        for g3 in STEP3_ORDER[:-1]:
-            multiply_step3(g3, 0)
-
-        def last_half(b):
-            accs_i = []
-            for i in range(V_TILES):
-                acc_i = step2.tile([P, HALF], F32, tag="acc")
-                multiply(acc_i[:], last_head, b, i)
-                accs_i.append(acc_i)
-            for i in range(V_TILES):
-                t = V_TILES * (last_head % HEADS_PER_PASS) + i
-                copy = nc.scalar.copy if i == 0 else nc.vector.tensor_copy
-                copy(
-                    out=result_half(last_head, b)[:, t, :].rearrange("p (r j) -> p r j", j=2),
-                    in_=accs_i[i][:].rearrange("p (j r) -> p r j", j=2),
-                )
-            store_half(last_head, b)
-
-        last_half(0)
-        for g3 in STEP3_ORDER[:-1]:
-            multiply_step3(g3, 1)
-        regroup(last_g3, 0)
-        last_half(1)
-        quantise_etc_v(last_g3, 0)
-        multiply_step3(last_g3, 0)
-        regroup(last_g3, 1)
-        finish_step3(0)
-        quantise_etc_v(last_g3, 1)
-        multiply_step3(last_g3, 1)
-        finish_step3(1)
+            if n + AHEAD < len(units):
+                transpose_unit(n + AHEAD)
+            run_due("tensor", n)
+            group_unit(n)
+            run_due("scalar", n)
+            quantise_unit(n)
+            run_due("vector", n)
+        for g3 in STEP3_ORDER[2:]:
+            for b in range(2):
+                multiply_step3(g3, b)
+        for b in range(2):
+            finish_step3(b)

@@ -28,7 +28,9 @@ HEADS_PER_PASS = K_PASS // CHANNELS
 UNIT_ROWS = 2 * P
 V_TILES = CHANNELS // P
 O_TILES = OUT_CHANNELS // P
+E_TILES = SLOTS // P
 HALF = SLOTS // 2
+MASK_ROWS = POSITIONS // (2 * P)
 HEAD_ORDER = [2, 3, 0, 1, 4, 5, 6, 7]
 STEP3_ORDER = [1, 0, 2, 3]
 UNITS_PER_HEAD = 6
@@ -43,7 +45,6 @@ def tile_block_pa_kernel(tc, v, e_s, mask, regular, re_w, re_b, out_0, out_1):
         ctx.enter_context(tc.manual_schedule())
         once = ctx.enter_context(tc.tile_pool(name="once", bufs=1))
         inputs = ctx.enter_context(tc.tile_pool(name="inputs", bufs=HEADS))
-        e_inputs = ctx.enter_context(tc.tile_pool(name="e_inputs", bufs=2 * HEADS))
         grouping = ctx.enter_context(tc.tile_pool(name="grouping", bufs=10))
         operands = ctx.enter_context(tc.tile_pool(name="operands", bufs=3))
         results = ctx.enter_context(tc.tile_pool(name="results", bufs=CHANNEL_PASSES))
@@ -51,20 +52,23 @@ def tile_block_pa_kernel(tc, v, e_s, mask, regular, re_w, re_b, out_0, out_1):
         step2 = ctx.enter_context(tc.psum_pool(name="step2", bufs=2))
 
         identity = once.tile([P, P], F32)
+        small_rows = once.tile([P, 2 * P], BF16)
+        nc.gpsimd.memset(small_rows[:], 0.0)
         make_identity(nc, identity[:])
 
         v_rows = {}
         e_rows = {}
-        mask_sb = once.tile([P, POSITION_PASSES, HALVES, PAIR], BF16)
         regular_sb = once.tile([P, 1], BF16)
         for place in range(HEADS):
             h = HEAD_ORDER[place]
             if place == 1:
                 nc.sync.dma_start(
-                    out=mask_sb[:],
-                    in_=mask[0, 0].rearrange(
-                        "(g u p e) -> p g u e", g=POSITION_PASSES, u=HALVES, e=PAIR
-                    ),
+                    out=small_rows[0:MASK_ROWS, :],
+                    in_=mask[0, 0].rearrange("(q w) -> q w", q=MASK_ROWS),
+                )
+                nc.sync.dma_start(
+                    out=small_rows[MASK_ROWS : MASK_ROWS + 1, :],
+                    in_=re_b.rearrange("(q w) -> q w", q=1),
                 )
                 nc.sync.dma_start(out=regular_sb[:], in_=regular.partition_broadcast(P))
             v_head = inputs.tile([P, V_TILES, POSITIONS], BF16)
@@ -78,19 +82,25 @@ def tile_block_pa_kernel(tc, v, e_s, mask, regular, re_w, re_b, out_0, out_1):
             else:
                 nc.sync.dma_start(out=v_head[:], in_=v_source)
             v_rows[h] = v_head
-            for b in range(2):
-                e_half = e_inputs.tile([P, 2, POSITIONS], BF16)
-                nc.sync.dma_start(
-                    out=e_half[:],
-                    in_=e_s[h, 0, b * HALF : (b + 1) * HALF, :].rearrange(
-                        "(p j) s -> p j s", j=2
-                    ),
-                )
-                e_rows[h, b] = e_half
+            e_head = inputs.tile([P, E_TILES, POSITIONS], BF16)
+            e_source = e_s[h, 0].rearrange("(p j) s -> p j s", j=E_TILES)
+            if place < 2:
+                for b in range(2):
+                    tiles = slice(2 * b, 2 * b + 2)
+                    nc.sync.dma_start(out=e_head[:, tiles, :], in_=e_source[:, tiles, :])
+            elif place == HEADS - 1:
+                for b in range(2):
+                    nc.sync.dma_start(
+                        out=e_head[:, 2 * b : 2 * b + 2, :],
+                        in_=e_s[h, 0, b * HALF : (b + 1) * HALF, :].rearrange(
+                            "(p j) s -> p j s", j=2
+                        ),
+                    )
+            else:
+                nc.sync.dma_start(out=e_head[:], in_=e_source)
+            e_rows[h] = e_head
         w_rows = once.tile([P, O_TILES, ALL_CHANNELS], BF16)
         nc.sync.dma_start(out=w_rows[:], in_=re_w.rearrange("(p m) c -> p m c", m=O_TILES))
-        bias_sb = once.tile([P, O_TILES], BF16)
-        nc.sync.dma_start(out=bias_sb[:], in_=re_b.rearrange("(p m) -> p m", m=O_TILES))
 
         regular_f32 = once.tile([P, 1], F32)
         factor = once.tile([P, POSITION_PASSES, HALVES, PAIR], F32)
@@ -118,8 +128,12 @@ def tile_block_pa_kernel(tc, v, e_s, mask, regular, re_w, re_b, out_0, out_1):
 
         def transpose_unit(n):
             kind, h, b, g = units[n]
-            rows = v_rows[h] if kind == "v" else e_rows[h, b] if kind == "e" else w_rows
-            words = rows[:].bitcast(F32)
+            if kind == "v":
+                words = v_rows[h][:].bitcast(F32)
+            elif kind == "e":
+                words = e_rows[h][:, 2 * b : 2 * b + 2, :].bitcast(F32)
+            else:
+                words = w_rows[:].bitcast(F32)
             bank = banks.tile([P, HALVES, UNIT_ROWS], F32, tag="bank")
             for u in range(HALVES):
                 block = slice((HALVES * g + u) * P, (HALVES * g + u + 1) * P)
@@ -173,10 +187,9 @@ def tile_block_pa_kernel(tc, v, e_s, mask, regular, re_w, re_b, out_0, out_1):
                 columns = slice(b * HALF, (b + 1) * HALF)
                 quantise(grouped_units[n], e_codes[:, g, columns], e_scales[:, g, columns])
 
-        def multiply(out, h, b, i):
+        def multiply(out, h, i, columns):
             v_codes, v_scales, e_codes, e_scales = head_operands[h]
             rows = slice(i * P, (i + 1) * P)
-            columns = slice(b * HALF, (b + 1) * HALF)
             for g in range(POSITION_PASSES):
                 nc.tensor.matmul_mx(
                     out=out,
@@ -188,70 +201,73 @@ def tile_block_pa_kernel(tc, v, e_s, mask, regular, re_w, re_b, out_0, out_1):
                     stop=(g == POSITION_PASSES - 1),
                 )
 
-        def multiply_half(h, b):
-            acc = step2.tile([P, V_TILES, HALF], F32, tag="acc")
-            for i in range(V_TILES):
-                multiply(acc[:, i, :], h, b, i)
-            accs[h, b] = acc
+        def multiply_tile(h, i):
+            acc = step2.tile([P, SLOTS], F32, tag="acc")
+            multiply(acc[:], h, i, slice(0, SLOTS))
+            accs[h, i] = acc
 
-        def multiply_half_apart(h, b):
+        def multiply_half(h, b):
             for i in range(V_TILES):
                 acc = step2.tile([P, HALF], F32, tag="acc")
-                multiply(acc[:], h, b, i)
+                multiply(acc[:], h, i, slice(b * HALF, (b + 1) * HALF))
                 accs[h, b, i] = acc
 
-        def result_half(h, b):
-            g3 = h // HEADS_PER_PASS
+        def result(g3):
             if g3 not in results_of_pass:
                 if g3 == STEP3_ORDER[-1]:
-                    low = once.tile([P, PACK, HALF], F32)
-                    high = once.tile([P, PACK, HALF], F32)
-                    results_of_pass[g3] = (low, high)
+                    last_pair = once.tile([P, 2, PACK, HALF], F32)
+                    results_of_pass[g3] = last_pair
                 else:
-                    whole = results.tile([P, PACK, SLOTS], F32)
-                    results_of_pass[g3] = (whole,)
+                    pair = results.tile([P, PACK, SLOTS], F32)
+                    results_of_pass[g3] = pair
+            return results_of_pass[g3]
+
+        def copy_out(copy, h, i):
+            g3, u = divmod(h, HEADS_PER_PASS)
+            t = V_TILES * u + i
             if g3 == STEP3_ORDER[-1]:
-                return results_of_pass[g3][b][:]
-            return results_of_pass[g3][0][:, :, b * HALF : (b + 1) * HALF]
+                copy(
+                    out=result(g3)[:, :, t, :].rearrange("p b (r j) -> p b r j", j=E_TILES),
+                    in_=accs[h, i][:].rearrange("p (j b r) -> p b r j", j=E_TILES, b=2),
+                )
+            else:
+                copy(
+                    out=result(g3)[:, t, :].rearrange("p (r j) -> p r j", j=E_TILES),
+                    in_=accs[h, i][:].rearrange("p (j r) -> p r j", j=E_TILES),
+                )
 
-        def copy_out(copy, h, b):
-            first = V_TILES * (h % HEADS_PER_PASS)
+        def copy_out_half(copy, h, b, i):
+            g3, u = divmod(h, HEADS_PER_PASS)
             copy(
-                out=result_half(h, b)[:, first : first + V_TILES, :].rearrange(
-                    "p i (r j) -> p i r j", j=2
-                ),
-                in_=accs[h, b][:].rearrange("p i (j r) -> p i r j", j=2),
-            )
-
-        def copy_out_tile(copy, h, b, i):
-            t = V_TILES * (h % HEADS_PER_PASS) + i
-            copy(
-                out=result_half(h, b)[:, t, :].rearrange("p (r j) -> p r j", j=2),
+                out=result(g3)[:, b, V_TILES * u + i, :].rearrange("p (r j) -> p r j", j=2),
                 in_=accs[h, b, i][:].rearrange("p (j r) -> p r j", j=2),
             )
 
         def store_head(h):
-            first = V_TILES * (h % HEADS_PER_PASS)
+            g3, u = divmod(h, HEADS_PER_PASS)
+            mine = slice(V_TILES * u, V_TILES * (u + 1))
             nc.sync.dma_start(
                 out=out_0[0, h].rearrange("(p i) e -> p i e", i=V_TILES),
-                in_=results_of_pass[h // HEADS_PER_PASS][0][:, first : first + V_TILES, :],
+                in_=result(g3)[:, mine, :],
             )
 
         def store_half(h, b):
-            first = V_TILES * (h % HEADS_PER_PASS)
+            g3, u = divmod(h, HEADS_PER_PASS)
+            mine = slice(V_TILES * u, V_TILES * (u + 1))
             nc.sync.dma_start(
                 out=out_0[0, h].rearrange("(p i) e -> p i e", i=V_TILES)[
                     :, :, b * HALF : (b + 1) * HALF
                 ],
-                in_=result_half(h, b)[:, first : first + V_TILES, :],
+                in_=result(g3)[:, b, mine, :],
             )
 
         def regroup(g3, b):
             half_grouped = results.tile([P, HALF, PACK], BF16, align_bytes=64)
-            nc.vector.tensor_copy(
-                out=half_grouped[:],
-                in_=result_half(g3 * HEADS_PER_PASS, b).rearrange("p t e -> p e t"),
-            )
+            if g3 == STEP3_ORDER[-1]:
+                values = result(g3)[:, b, :, :]
+            else:
+                values = result(g3)[:, :, b * HALF : (b + 1) * HALF]
+            nc.vector.tensor_copy(out=half_grouped[:], in_=values.rearrange("p t e -> p e t"))
             grouped_etc_v[g3, b] = half_grouped
 
         def quantise_etc_v(g3, b):
@@ -293,12 +309,21 @@ def tile_block_pa_kernel(tc, v, e_s, mask, regular, re_w, re_b, out_0, out_1):
                 in_=etc_k_sb[:, :, columns],
             )
 
-        def make_factor():
+        def transpose_small():
+            small_bank = banks.tile([P, P], F32, tag="bank")
+            nc.tensor.transpose(small_bank[:], small_rows[:].bitcast(F32), identity[:])
+            flipped["small"] = small_bank
+
+        def take_small():
+            values = flipped["small"][:].bitcast(BF16)
             nc.scalar.activation(
-                out=factor[:],
-                in_=mask_sb[:],
+                out=factor[:].rearrange("p g u e -> p (g u e)"),
+                in_=values[:, 0 : MASK_ROWS * PAIR],
                 func=mybir.ActivationFunctionType.Copy,
                 scale=regular_f32[:, 0:1],
+            )
+            nc.scalar.copy(
+                out=bias_f32[:], in_=values[:, MASK_ROWS * PAIR : (MASK_ROWS + 1) * PAIR]
             )
 
         due = {}
@@ -316,16 +341,16 @@ def tile_block_pa_kernel(tc, v, e_s, mask, regular, re_w, re_b, out_0, out_1):
             end = UNITS_PER_HEAD * (place + 1)
             if place == HEADS - 1:
                 for b in range(2):
-                    later("tensor", end - 1 + b, multiply_half_apart, h, b)
-                    later("scalar", end + b, copy_out_tile, nc.scalar.copy, h, b, 0)
-                    later("vector", end - 1 + b, copy_out_tile, nc.vector.tensor_copy, h, b, 1)
+                    later("tensor", end - 1 + b, multiply_half, h, b)
+                    later("scalar", end + b, copy_out_half, nc.scalar.copy, h, b, 0)
+                    later("vector", end - 1 + b, copy_out_half, nc.vector.tensor_copy, h, b, 1)
                     later("vector", end + b, store_half, h, b)
                     later("vector", end + b, regroup, g3, b)
                     later("vector", end + 2 + b, quantise_etc_v, g3, b)
                 continue
-            for b in range(2):
-                later("tensor", end - 1 + 3 * b, multiply_half, h, b)
-            later("scalar", end + 1, copy_out, nc.scalar.copy, h, 0)
+            for i in range(V_TILES):
+                later("tensor", end + 2 * i, multiply_tile, h, i)
+            later("scalar", end + 2, copy_out, nc.scalar.copy, h, 0)
             if place < 2:
                 later("scalar", end + 4, copy_out, nc.scalar.copy, h, 1)
             else:
@@ -341,8 +366,8 @@ def tile_block_pa_kernel(tc, v, e_s, mask, regular, re_w, re_b, out_0, out_1):
                     later("vector", end + 6 + 2 * b, quantise_etc_v, g3, b)
         head0_first = units.index(("v", 0, 0, 0))
         later("vector", head0_first - 4, nc.vector.tensor_copy, regular_f32[:], regular_sb[:])
-        later("scalar", head0_first - 2, make_factor)
-        later("vector", first_w, nc.vector.tensor_copy, bias_f32[:], bias_sb[:])
+        later("tensor", head0_first - 4, transpose_small)
+        later("scalar", head0_first - 2, take_small)
         for b in range(2):
             later("tensor", first_w + 2, multiply_step3, STEP3_ORDER[0], b)
             later("tensor", first_w + 3, multiply_step3, STEP3_ORDER[1], b)

@@ -31,8 +31,8 @@ O_TILES = OUT_CHANNELS // P
 E_TILES = SLOTS // P
 HALF = SLOTS // 2
 MASK_ROWS = POSITIONS // (2 * P)
-HEAD_ORDER = [2, 3, 0, 1, 4, 5, 6, 7]
-STEP3_ORDER = [1, 0, 2, 3]
+HEAD_ORDER = [1, 0, 2, 3, 4, 5, 6, 7]
+STEP3_ORDER = [0, 1, 2, 3]
 UNITS_PER_HEAD = 6
 AHEAD = 3
 
@@ -349,24 +349,24 @@ def tile_block_pa_kernel(tc, v, e_s, mask, regular, re_w, re_b, out_0, out_1):
                     later("vector", end + 2 + b, quantise_etc_v, g3, b)
                 continue
             for i in range(V_TILES):
-                later("tensor", end + 2 * i, multiply_tile, h, i)
-            later("scalar", end + 2, copy_out, nc.scalar.copy, h, 0)
-            if place < 2:
-                later("scalar", end + 4, copy_out, nc.scalar.copy, h, 1)
-            else:
-                later("vector", end + 4, copy_out, nc.vector.tensor_copy, h, 1)
+                later("tensor", end + 3 * i, multiply_tile, h, i)
+            for i in range(V_TILES):
+                if (i == 1 or place < 2) and place < HEADS - 2:
+                    later("vector", end + 2 + 3 * i, copy_out, nc.vector.tensor_copy, h, i)
+                else:
+                    later("scalar", end + 2 + 3 * i, copy_out, nc.scalar.copy, h, i)
             if g3 == STEP3_ORDER[-1]:
                 for b in range(2):
-                    later("vector", end + 4, store_half, h, b)
+                    later("vector", end + 5, store_half, h, b)
             else:
-                later("vector", end + 4, store_head, h)
+                later("vector", end + 5, store_head, h)
             if place % HEADS_PER_PASS == HEADS_PER_PASS - 1:
                 for b in range(2):
-                    later("vector", end + 5 + 2 * b, regroup, g3, b)
-                    later("vector", end + 6 + 2 * b, quantise_etc_v, g3, b)
+                    later("vector", end + 6 + 2 * b, regroup, g3, b)
+                    later("vector", end + 7 + 2 * b, quantise_etc_v, g3, b)
         head0_first = units.index(("v", 0, 0, 0))
-        later("vector", head0_first - 4, nc.vector.tensor_copy, regular_f32[:], regular_sb[:])
-        later("tensor", head0_first - 4, transpose_small)
+        later("vector", head0_first - 3, nc.vector.tensor_copy, regular_f32[:], regular_sb[:])
+        later("tensor", head0_first - 3, transpose_small)
         later("scalar", head0_first - 2, take_small)
         for b in range(2):
             later("tensor", first_w + 2, multiply_step3, STEP3_ORDER[0], b)
@@ -380,6 +380,10 @@ def tile_block_pa_kernel(tc, v, e_s, mask, regular, re_w, re_b, out_0, out_1):
             run_due("tensor", n)
             group_unit(n)
             run_due("scalar", n)
+            if n == head0_first:
+                continue
+            if n == head0_first + 1:
+                quantise_unit(head0_first)
             quantise_unit(n)
             run_due("vector", n)
         for g3 in STEP3_ORDER[2:]:

@@ -84,7 +84,7 @@ def tile_block_pa_kernel(tc, v, e_s, mask, regular, re_w, re_b, out_0, out_1):
             v_rows[h] = v_head
             e_head = inputs.tile([P, E_TILES, POSITIONS], BF16)
             e_source = e_s[h, 0].rearrange("(p j) s -> p j s", j=E_TILES)
-            if place < 2:
+            if place < HEADS // 2:
                 for b in range(2):
                     tiles = slice(2 * b, 2 * b + 2)
                     nc.sync.dma_start(out=e_head[:, tiles, :], in_=e_source[:, tiles, :])
@@ -207,10 +207,10 @@ def tile_block_pa_kernel(tc, v, e_s, mask, regular, re_w, re_b, out_0, out_1):
             accs[h, i] = acc
 
         def multiply_half(h, b):
+            acc = step2.tile([P, V_TILES, HALF], F32, tag="acc")
             for i in range(V_TILES):
-                acc = step2.tile([P, HALF], F32, tag="acc")
-                multiply(acc[:], h, i, slice(b * HALF, (b + 1) * HALF))
-                accs[h, b, i] = acc
+                multiply(acc[:, i, :], h, i, slice(b * HALF, (b + 1) * HALF))
+            accs[h, "half", b] = acc
 
         def result(g3):
             if g3 not in results_of_pass:
@@ -236,11 +236,13 @@ def tile_block_pa_kernel(tc, v, e_s, mask, regular, re_w, re_b, out_0, out_1):
                     in_=accs[h, i][:].rearrange("p (j r) -> p r j", j=E_TILES),
                 )
 
-        def copy_out_half(copy, h, b, i):
+        def copy_out_half(h, b):
             g3, u = divmod(h, HEADS_PER_PASS)
-            copy(
-                out=result(g3)[:, b, V_TILES * u + i, :].rearrange("p (r j) -> p r j", j=2),
-                in_=accs[h, b, i][:].rearrange("p (j r) -> p r j", j=2),
+            nc.scalar.copy(
+                out=result(g3)[:, b, V_TILES * u : V_TILES * (u + 1), :].rearrange(
+                    "p i (r j) -> p i r j", j=2
+                ),
+                in_=accs[h, "half", b][:].rearrange("p i (j r) -> p i r j", j=2),
             )
 
         def store_head(h):
@@ -342,8 +344,7 @@ def tile_block_pa_kernel(tc, v, e_s, mask, regular, re_w, re_b, out_0, out_1):
             if place == HEADS - 1:
                 for b in range(2):
                     later("tensor", end - 1 + b, multiply_half, h, b)
-                    later("scalar", end + b, copy_out_half, nc.scalar.copy, h, b, 0)
-                    later("vector", end - 1 + b, copy_out_half, nc.vector.tensor_copy, h, b, 1)
+                    later("scalar", end + b, copy_out_half, h, b)
                     later("vector", end + b, store_half, h, b)
                     later("vector", end + b, regroup, g3, b)
                     later("vector", end + 2 + b, quantise_etc_v, g3, b)
@@ -363,7 +364,7 @@ def tile_block_pa_kernel(tc, v, e_s, mask, regular, re_w, re_b, out_0, out_1):
             if place % HEADS_PER_PASS == HEADS_PER_PASS - 1:
                 for b in range(2):
                     later("vector", end + 6 + 2 * b, regroup, g3, b)
-                    later("vector", end + 7 + 2 * b, quantise_etc_v, g3, b)
+                    later("vector", end + 8 + 2 * b, quantise_etc_v, g3, b)
         head0_first = units.index(("v", 0, 0, 0))
         later("vector", head0_first - 3, nc.vector.tensor_copy, regular_f32[:], regular_sb[:])
         later("tensor", head0_first - 3, transpose_small)

@@ -34,6 +34,7 @@ MASK_ROWS = POSITIONS // (2 * P)
 HEAD_ORDER = [1, 0, 2, 3, 4, 5, 6, 7]
 STEP3_ORDER = [0, 1, 2, 3]
 UNITS_PER_HEAD = 6
+RUN = 4
 AHEAD = 3
 
 FLOPS = 2 * HEADS * CHANNELS * SLOTS * POSITIONS + 2 * OUT_CHANNELS * ALL_CHANNELS * SLOTS
@@ -269,7 +270,10 @@ def tile_block_pa_kernel(tc, v, e_s, mask, regular, re_w, re_b, out_0, out_1):
                 values = result(g3)[:, b, :, :]
             else:
                 values = result(g3)[:, :, b * HALF : (b + 1) * HALF]
-            nc.vector.tensor_copy(out=half_grouped[:], in_=values.rearrange("p t e -> p e t"))
+            nc.vector.tensor_copy(
+                out=half_grouped[:].rearrange("p (c i) t -> p c t i", i=RUN),
+                in_=values.rearrange("p t (c i) -> p c t i", i=RUN),
+            )
             grouped_etc_v[g3, b] = half_grouped
 
         def quantise_etc_v(g3, b):

@@ -55,7 +55,14 @@ def tile_block_pa_kernel(tc, v, e_s, mask, regular, re_w, re_b, out_0, out_1):
         identity = once.tile([P, P], F32)
         small_rows = once.tile([P, 2 * P], BF16)
         nc.gpsimd.memset(small_rows[:], 0.0)
+        warm = once.tile([P, SLOTS], BF16)
+        nc.vector.memset(warm[:], 0.0)
         make_identity(nc, identity[:])
+        scrap = step2.tile([P, SLOTS], F32, tag="acc")
+
+        def keep_warm():
+            nc.tensor.matmul(scrap[:], lhsT=warm[:, 0:P], rhs=warm[:], start=True, stop=True)
+
 
         v_rows = {}
         e_rows = {}
@@ -357,9 +364,9 @@ def tile_block_pa_kernel(tc, v, e_s, mask, regular, re_w, re_b, out_0, out_1):
                 later("tensor", end + 3 * i, multiply_tile, h, i)
             for i in range(V_TILES):
                 if (i == 1 or place < 2) and place < HEADS - 2:
-                    later("vector", end + 2 + 3 * i, copy_out, nc.vector.tensor_copy, h, i)
+                    later("vector", end + 3 + 2 * i, copy_out, nc.vector.tensor_copy, h, i)
                 else:
-                    later("scalar", end + 2 + 3 * i, copy_out, nc.scalar.copy, h, i)
+                    later("scalar", end + 3 + 2 * i, copy_out, nc.scalar.copy, h, i)
             if g3 == STEP3_ORDER[-1]:
                 for b in range(2):
                     later("vector", end + 5, store_half, h, b)
@@ -377,11 +384,16 @@ def tile_block_pa_kernel(tc, v, e_s, mask, regular, re_w, re_b, out_0, out_1):
             later("tensor", first_w + 2, multiply_step3, STEP3_ORDER[0], b)
             later("tensor", first_w + 3, multiply_step3, STEP3_ORDER[1], b)
 
+        for n in range(7):
+            keep_warm()
         for n in range(AHEAD):
             transpose_unit(n)
+            keep_warm()
         for n in range(len(units)):
             if n + AHEAD < len(units):
                 transpose_unit(n + AHEAD)
+            if n == 0:
+                keep_warm()
             run_due("tensor", n)
             group_unit(n)
             run_due("scalar", n)

@@ -363,7 +363,7 @@ def tile_block_pa_kernel(tc, v, e_s, mask, regular, re_w, re_b, out_0, out_1):
             for i in range(V_TILES):
                 later("tensor", end + 3 * i, multiply_tile, h, i)
             for i in range(V_TILES):
-                if (i == 1 or place < 2) and place < HEADS - 2:
+                if (i == 1 or place % HEADS_PER_PASS == 1) and place < HEADS - 2:
                     later("vector", end + 3 + 2 * i, copy_out, nc.vector.tensor_copy, h, i)
                 else:
                     later("scalar", end + 3 + 2 * i, copy_out, nc.scalar.copy, h, i)
@@ -374,11 +374,11 @@ def tile_block_pa_kernel(tc, v, e_s, mask, regular, re_w, re_b, out_0, out_1):
                 later("vector", end + 5, store_head, h)
             if place % HEADS_PER_PASS == HEADS_PER_PASS - 1:
                 for b in range(2):
-                    later("vector", end + 6 + 2 * b, regroup, g3, b)
-                    later("vector", end + 8 + 2 * b, quantise_etc_v, g3, b)
+                    later("vector", end + 7 + 2 * b, regroup, g3, b)
+                    later("vector", end + 9 + 2 * b, quantise_etc_v, g3, b)
         head0_first = units.index(("v", 0, 0, 0))
         later("vector", head0_first - 3, nc.vector.tensor_copy, regular_f32[:], regular_sb[:])
-        later("tensor", head0_first - 3, transpose_small)
+        later("tensor", head0_first - 4, transpose_small)
         later("scalar", head0_first - 2, take_small)
         for b in range(2):
             later("tensor", first_w + 2, multiply_step3, STEP3_ORDER[0], b)

@@ -83,12 +83,7 @@ def tile_block_pa_kernel(tc, v, e_s, mask, regular, re_w, re_b, out_0, out_1):
             v_source = v[0, h * CHANNELS : (h + 1) * CHANNELS, :].rearrange(
                 "(p i) s -> p i s", i=V_TILES
             )
-            if place == 0:
-                for g in range(POSITION_PASSES):
-                    columns = slice(g * K_PASS, (g + 1) * K_PASS)
-                    nc.sync.dma_start(out=v_head[:, :, columns], in_=v_source[:, :, columns])
-            else:
-                nc.sync.dma_start(out=v_head[:], in_=v_source)
+            nc.sync.dma_start(out=v_head[:], in_=v_source)
             v_rows[h] = v_head
             e_head = inputs.tile([P, E_TILES, POSITIONS], BF16)
             e_source = e_s[h, 0].rearrange("(p j) s -> p j s", j=E_TILES)
@@ -317,10 +312,6 @@ def tile_block_pa_kernel(tc, v, e_s, mask, regular, re_w, re_b, out_0, out_1):
             nc.vector.tensor_scalar_add(
                 out=etc_k_sb[:, 1, columns], in0=etc_k_acc[1, b][:], scalar1=bias_f32[:, 1:2]
             )
-            nc.sync.dma_start(
-                out=out_1[0].rearrange("(p m) e -> p m e", m=O_TILES)[:, :, columns],
-                in_=etc_k_sb[:, :, columns],
-            )
 
         def transpose_small():
             small_bank = banks.tile([P, P], F32, tag="bank")
@@ -361,12 +352,12 @@ def tile_block_pa_kernel(tc, v, e_s, mask, regular, re_w, re_b, out_0, out_1):
                     later("vector", end + 2 + b, quantise_etc_v, g3, b)
                 continue
             for i in range(V_TILES):
-                later("tensor", end + 3 * i, multiply_tile, h, i)
+                later("tensor", end + 2, multiply_tile, h, i)
             for i in range(V_TILES):
                 if (i == 1 or place % HEADS_PER_PASS == 1) and place < HEADS - 2:
-                    later("vector", end + 3 + 2 * i, copy_out, nc.vector.tensor_copy, h, i)
+                    later("vector", end + 4 + i, copy_out, nc.vector.tensor_copy, h, i)
                 else:
-                    later("scalar", end + 3 + 2 * i, copy_out, nc.scalar.copy, h, i)
+                    later("scalar", end + 4 + i, copy_out, nc.scalar.copy, h, i)
             if g3 == STEP3_ORDER[-1]:
                 for b in range(2):
                     later("vector", end + 5, store_half, h, b)
@@ -408,3 +399,4 @@ def tile_block_pa_kernel(tc, v, e_s, mask, regular, re_w, re_b, out_0, out_1):
                 multiply_step3(g3, b)
         for b in range(2):
             finish_step3(b)
+        nc.sync.dma_start(out=out_1[0].rearrange("(p m) e -> p m e", m=O_TILES), in_=etc_k_sb[:])

from contextlib import ExitStack

import concourse.mybir as mybir
from concourse.masks import make_identity

BF16 = mybir.dt.bfloat16
F32 = mybir.dt.float32
U32 = mybir.dt.uint32
U8 = mybir.dt.uint8
FP8X4 = mybir.dt.float8_e4m3fn_x4

P = 128
PACK = 4
K_PASS = P * PACK
HALVES = 2
PAIR = 2

HEADS = 8
CHANNELS = 256
SLOTS = 512
POSITIONS = 1024
ALL_CHANNELS = HEADS * CHANNELS
OUT_CHANNELS = 256

POSITION_PASSES = POSITIONS // K_PASS
CHANNEL_PASSES = ALL_CHANNELS // K_PASS
HEADS_PER_PASS = K_PASS // CHANNELS
UNIT_ROWS = 2 * P
V_TILES = CHANNELS // P
O_TILES = OUT_CHANNELS // P
E_TILES = SLOTS // P
HALF = SLOTS // 2
MASK_ROWS = POSITIONS // (2 * P)
HEAD_ORDER = [1, 0, 2, 3, 4, 5, 6, 7]
STEP3_ORDER = [0, 1, 2, 3]
UNITS_PER_HEAD = 6
RUN = 4
AHEAD = 3

FLOPS = 2 * HEADS * CHANNELS * SLOTS * POSITIONS + 2 * OUT_CHANNELS * ALL_CHANNELS * SLOTS


def tile_block_pa_kernel(tc, v, e_s, mask, regular, re_w, re_b, out_0, out_1):
    nc = tc.nc
    with ExitStack() as ctx:
        ctx.enter_context(tc.manual_schedule())
        once = ctx.enter_context(tc.tile_pool(name="once", bufs=1))
        inputs = ctx.enter_context(tc.tile_pool(name="inputs", bufs=HEADS))
        grouping = ctx.enter_context(tc.tile_pool(name="grouping", bufs=10))
        operands = ctx.enter_context(tc.tile_pool(name="operands", bufs=3))
        results = ctx.enter_context(tc.tile_pool(name="results", bufs=CHANNEL_PASSES))
        banks = ctx.enter_context(tc.psum_pool(name="banks", bufs=6))
        step2 = ctx.enter_context(tc.psum_pool(name="step2", bufs=2))

        identity = once.tile([P, P], F32)
        small_rows = once.tile([P, 2 * P], BF16)
        nc.gpsimd.memset(small_rows[:], 0.0)
        warm = once.tile([P, SLOTS], BF16)
        nc.vector.memset(warm[:], 0.0)
        make_identity(nc, identity[:])
        scrap = step2.tile([P, SLOTS], F32, tag="acc")

        def keep_warm():
            nc.tensor.matmul(scrap[:], lhsT=warm[:, 0:P], rhs=warm[:], start=True, stop=True)


        v_rows = {}
        e_rows = {}
        regular_sb = once.tile([P, 1], BF16)
        for place in range(HEADS):
            h = HEAD_ORDER[place]
            if place == 1:
                nc.sync.dma_start(
                    out=small_rows[0:MASK_ROWS, :],
                    in_=mask[0, 0].rearrange("(q w) -> q w", q=MASK_ROWS),
                )
                nc.sync.dma_start(
                    out=small_rows[MASK_ROWS : MASK_ROWS + 1, :],
                    in_=re_b.rearrange("(q w) -> q w", q=1),
                )
                nc.sync.dma_start(out=regular_sb[:], in_=regular.partition_broadcast(P))
            v_head = inputs.tile([P, V_TILES, POSITIONS], BF16)
            v_source = v[0, h * CHANNELS : (h + 1) * CHANNELS, :].rearrange(
                "(p i) s -> p i s", i=V_TILES
            )
            nc.sync.dma_start(out=v_head[:], in_=v_source)
            v_rows[h] = v_head
            e_head = inputs.tile([P, E_TILES, POSITIONS], BF16)
            e_source = e_s[h, 0].rearrange("(p j) s -> p j s", j=E_TILES)
            if place < HEADS // 2:
                for b in range(2):
                    tiles = slice(2 * b, 2 * b + 2)
                    nc.sync.dma_start(out=e_head[:, tiles, :], in_=e_source[:, tiles, :])
            elif place == HEADS - 1:
                for b in range(2):
                    nc.sync.dma_start(
                        out=e_head[:, 2 * b : 2 * b + 2, :],
                        in_=e_s[h, 0, b * HALF : (b + 1) * HALF, :].rearrange(
                            "(p j) s -> p j s", j=2
                        ),
                    )
            else:
                nc.sync.dma_start(out=e_head[:], in_=e_source)
            e_rows[h] = e_head
        w_rows = once.tile([P, O_TILES, ALL_CHANNELS], BF16)
        nc.sync.dma_start(out=w_rows[:], in_=re_w.rearrange("(p m) c -> p m c", m=O_TILES))

        regular_f32 = once.tile([P, 1], F32)
        factor = once.tile([P, POSITION_PASSES, HALVES, PAIR], F32)
        bias_f32 = once.tile([P, O_TILES], F32)
        w_codes = once.tile([P, CHANNEL_PASSES, OUT_CHANNELS], U32, align_bytes=64)
        w_scales = once.tile([P, CHANNEL_PASSES, OUT_CHANNELS], U8, align_bytes=64)
        etc_v_codes = once.tile([P, CHANNEL_PASSES, SLOTS], U32, align_bytes=64)
        etc_v_scales = once.tile([P, CHANNEL_PASSES, SLOTS], U8, align_bytes=64)
        etc_k_sb = once.tile([P, O_TILES, SLOTS], F32)
        head_operands = {}
        results_of_pass = {}
        flipped = {}
        grouped_units = {}
        accs = {}
        grouped_etc_v = {}
        etc_k_acc = {}

        units = []
        for h in HEAD_ORDER:
            units.extend([("v", h, 0, g) for g in range(POSITION_PASSES)])
            for b in range(2):
                units.extend([("e", h, b, g) for g in range(POSITION_PASSES)])
        first_w = len(units)
        units.extend([("w", 0, 0, g) for g in STEP3_ORDER])

        def transpose_unit(n):
            kind, h, b, g = units[n]
            if kind == "v":
                words = v_rows[h][:].bitcast(F32)
            elif kind == "e":
                words = e_rows[h][:, 2 * b : 2 * b + 2, :].bitcast(F32)
            else:
                words = w_rows[:].bitcast(F32)
            bank = banks.tile([P, HALVES, UNIT_ROWS], F32, tag="bank")
            for u in range(HALVES):
                block = slice((HALVES * g + u) * P, (HALVES * g + u + 1) * P)
                for i in range(2):
                    nc.tensor.transpose(
                        bank[:, u, i * P : (i + 1) * P], words[:, i, block], identity[:]
                    )
            flipped[n] = bank

        def group_unit(n):
            kind, h, b, g = units[n]
            bank = flipped[n]
            grouped = grouping.tile([P, UNIT_ROWS, PACK], BF16, align_bytes=64)
            if kind == "v" and h == 0:
                nc.vector.tensor_tensor(
                    out=grouped[:].rearrange("p c (u e) -> p c u e", e=PAIR),
                    in0=bank[:].bitcast(BF16).rearrange("p u (c e) -> p c u e", e=PAIR),
                    in1=factor[:, g, :, :]
                    .unsqueeze(1)
                    .to_broadcast([P, UNIT_ROWS, HALVES, PAIR]),
                    op=mybir.AluOpType.mult,
                )
            else:
                nc.scalar.copy(
                    out=grouped[:].bitcast(F32), in_=bank[:].rearrange("p u c -> p c u")
                )
            grouped_units[n] = grouped

        def quantise(grouped, codes, scales):
            nc.vector.quantize_mx(
                out=codes.bitcast(FP8X4),
                scales=scales,
                in_=grouped[:].rearrange("p c t -> p (c t)"),
            )

        def quantise_unit(n):
            kind, h, b, g = units[n]
            if kind == "w":
                quantise(grouped_units[n], w_codes[:, g, :], w_scales[:, g, :])
                return
            if h not in head_operands:
                v_codes = operands.tile([P, POSITION_PASSES, CHANNELS], U32, align_bytes=64)
                v_scales = operands.tile([P, POSITION_PASSES, CHANNELS], U8, align_bytes=64)
                e_codes = operands.tile([P, POSITION_PASSES, SLOTS], U32, align_bytes=64)
                e_scales = operands.tile([P, POSITION_PASSES, SLOTS], U8, align_bytes=64)
                head_operands[h] = (v_codes, v_scales, e_codes, e_scales)
            v_codes, v_scales, e_codes, e_scales = head_operands[h]
            if kind == "v":
                quantise(grouped_units[n], v_codes[:, g, :], v_scales[:, g, :])
            else:
                columns = slice(b * HALF, (b + 1) * HALF)
                quantise(grouped_units[n], e_codes[:, g, columns], e_scales[:, g, columns])

        def multiply(out, h, i, columns):
            v_codes, v_scales, e_codes, e_scales = head_operands[h]
            rows = slice(i * P, (i + 1) * P)
            for g in range(POSITION_PASSES):
                nc.tensor.matmul_mx(
                    out=out,
                    lhsT=v_codes[:, g, rows].bitcast(FP8X4),
                    lhsT_scale=v_scales[:, g, rows],
                    rhs=e_codes[:, g, columns].bitcast(FP8X4),
                    rhs_scale=e_scales[:, g, columns],
                    start=(g == 0),
                    stop=(g == POSITION_PASSES - 1),
                )

        def multiply_tile(h, i):
            acc = step2.tile([P, SLOTS], F32, tag="acc")
            multiply(acc[:], h, i, slice(0, SLOTS))
            accs[h, i] = acc

        def multiply_half(h, b):
            acc = step2.tile([P, V_TILES, HALF], F32, tag="acc")
            for i in range(V_TILES):
                multiply(acc[:, i, :], h, i, slice(b * HALF, (b + 1) * HALF))
            accs[h, "half", b] = acc

        def result(g3):
            if g3 not in results_of_pass:
                if g3 == STEP3_ORDER[-1]:
                    last_pair = once.tile([P, 2, PACK, HALF], F32)
                    results_of_pass[g3] = last_pair
                else:
                    pair = results.tile([P, PACK, SLOTS], F32)
                    results_of_pass[g3] = pair
            return results_of_pass[g3]

        def copy_out(copy, h, i):
            g3, u = divmod(h, HEADS_PER_PASS)
            t = V_TILES * u + i
            if g3 == STEP3_ORDER[-1]:
                copy(
                    out=result(g3)[:, :, t, :].rearrange("p b (r j) -> p b r j", j=E_TILES),
                    in_=accs[h, i][:].rearrange("p (j b r) -> p b r j", j=E_TILES, b=2),
                )
            else:
                copy(
                    out=result(g3)[:, t, :].rearrange("p (r j) -> p r j", j=E_TILES),
                    in_=accs[h, i][:].rearrange("p (j r) -> p r j", j=E_TILES),
                )

        def copy_out_half(h, b):
            g3, u = divmod(h, HEADS_PER_PASS)
            nc.scalar.copy(
                out=result(g3)[:, b, V_TILES * u : V_TILES * (u + 1), :].rearrange(
                    "p i (r j) -> p i r j", j=2
                ),
                in_=accs[h, "half", b][:].rearrange("p i (j r) -> p i r j", j=2),
            )

        def store_head(h):
            g3, u = divmod(h, HEADS_PER_PASS)
            mine = slice(V_TILES * u, V_TILES * (u + 1))
            nc.sync.dma_start(
                out=out_0[0, h].rearrange("(p i) e -> p i e", i=V_TILES),
                in_=result(g3)[:, mine, :],
            )

        def store_half(h, b):
            g3, u = divmod(h, HEADS_PER_PASS)
            mine = slice(V_TILES * u, V_TILES * (u + 1))
            nc.sync.dma_start(
                out=out_0[0, h].rearrange("(p i) e -> p i e", i=V_TILES)[
                    :, :, b * HALF : (b + 1) * HALF
                ],
                in_=result(g3)[:, b, mine, :],
            )

        def regroup(g3, b):
            half_grouped = results.tile([P, HALF, PACK], BF16, align_bytes=64)
            if g3 == STEP3_ORDER[-1]:
                values = result(g3)[:, b, :, :]
            else:
                values = result(g3)[:, :, b * HALF : (b + 1) * HALF]
            nc.vector.tensor_copy(
                out=half_grouped[:].rearrange("p (c i) t -> p c t i", i=RUN),
                in_=values.rearrange("p t (c i) -> p c t i", i=RUN),
            )
            grouped_etc_v[g3, b] = half_grouped

        def quantise_etc_v(g3, b):
            columns = slice(b * HALF, (b + 1) * HALF)
            quantise(
                grouped_etc_v[g3, b], etc_v_codes[:, g3, columns], etc_v_scales[:, g3, columns]
            )

        def multiply_step3(g3, b):
            columns = slice(b * HALF, (b + 1) * HALF)
            for m in range(O_TILES):
                if (m, b) not in etc_k_acc:
                    k_bank = banks.tile([P, HALF], F32, tag="bank")
                    etc_k_acc[m, b] = k_bank
                rows = slice(m * P, (m + 1) * P)
                nc.tensor.matmul_mx(
                    out=etc_k_acc[m, b][:],
                    lhsT=w_codes[:, g3, rows].bitcast(FP8X4),
                    lhsT_scale=w_scales[:, g3, rows],
                    rhs=etc_v_codes[:, g3, columns].bitcast(FP8X4),
                    rhs_scale=etc_v_scales[:, g3, columns],
                    start=(g3 == STEP3_ORDER[0]),
                    stop=(g3 == STEP3_ORDER[-1]),
                )

        def finish_step3(b):
            columns = slice(b * HALF, (b + 1) * HALF)
            nc.scalar.activation(
                out=etc_k_sb[:, 0, columns],
                in_=etc_k_acc[0, b][:],
                func=mybir.ActivationFunctionType.Identity,
                bias=bias_f32[:, 0:1],
            )
            nc.vector.tensor_scalar_add(
                out=etc_k_sb[:, 1, columns], in0=etc_k_acc[1, b][:], scalar1=bias_f32[:, 1:2]
            )

        def transpose_small():
            small_bank = banks.tile([P, P], F32, tag="bank")
            nc.tensor.transpose(small_bank[:], small_rows[:].bitcast(F32), identity[:])
            flipped["small"] = small_bank

        def take_small():
            values = flipped["small"][:].bitcast(BF16)
            nc.scalar.activation(
                out=factor[:].rearrange("p g u e -> p (g u e)"),
                in_=values[:, 0 : MASK_ROWS * PAIR],
                func=mybir.ActivationFunctionType.Copy,
                scale=regular_f32[:, 0:1],
            )
            nc.scalar.copy(
                out=bias_f32[:], in_=values[:, MASK_ROWS * PAIR : (MASK_ROWS + 1) * PAIR]
            )

        due = {}

        def later(engine, n, job, *args):
            due.setdefault((engine, n), []).append((job, args))

        def run_due(engine, n):
            for job, args in due.get((engine, n), []):
                job(*args)

        for place in range(HEADS):
            h = HEAD_ORDER[place]
            g3 = h // HEADS_PER_PASS
            end = UNITS_PER_HEAD * (place + 1)
            if place == HEADS - 1:
                for b in range(2):
                    later("tensor", end - 1 + b, multiply_half, h, b)
                    later("scalar", end + b, copy_out_half, h, b)
                    later("vector", end + b, store_half, h, b)
                    later("vector", end + b, regroup, g3, b)
                    later("vector", end + 2 + b, quantise_etc_v, g3, b)
                continue
            for i in range(V_TILES):
                later("tensor", end + 2, multiply_tile, h, i)
            for i in range(V_TILES):
                if (i == 1 or place % HEADS_PER_PASS == 1) and place < HEADS - 2:
                    later("vector", end + 4 + i, copy_out, nc.vector.tensor_copy, h, i)
                else:
                    later("scalar", end + 4 + i, copy_out, nc.scalar.copy, h, i)
            if g3 == STEP3_ORDER[-1]:
                for b in range(2):
                    later("vector", end + 5, store_half, h, b)
            else:
                later("vector", end + 5, store_head, h)
            if place % HEADS_PER_PASS == HEADS_PER_PASS - 1:
                for b in range(2):
                    later("vector", end + 7 + 2 * b, regroup, g3, b)
                    later("vector", end + 9 + 2 * b, quantise_etc_v, g3, b)
        head0_first = units.index(("v", 0, 0, 0))
        later("vector", head0_first - 3, nc.vector.tensor_copy, regular_f32[:], regular_sb[:])
        later("tensor", head0_first - 4, transpose_small)
        later("scalar", head0_first - 2, take_small)
        for b in range(2):
            later("tensor", first_w + 2, multiply_step3, STEP3_ORDER[0], b)
            later("tensor", first_w + 3, multiply_step3, STEP3_ORDER[1], b)

        for n in range(7):
            keep_warm()
        for n in range(AHEAD):
            transpose_unit(n)
            keep_warm()
        for n in range(len(units)):
            if n + AHEAD < len(units):
                transpose_unit(n + AHEAD)
            if n == 0:
                keep_warm()
            run_due("tensor", n)
            group_unit(n)
            run_due("scalar", n)
            if n == head0_first:
                continue
            if n == head0_first + 1:
                quantise_unit(head0_first)
            quantise_unit(n)
            run_due("vector", n)
        for g3 in STEP3_ORDER[2:]:
            for b in range(2):
                multiply_step3(g3, b)
        for b in range(2):
            finish_step3(b)
        nc.sync.dma_start(out=out_1[0].rearrange("(p m) e -> p m e", m=O_TILES), in_=etc_k_sb[:])
